import numpy as np
import ml_dtypes


def mxq(x, axis, fmt="e4m3"):
    dtype, down = {"e4m3": (ml_dtypes.float8_e4m3fn, 7), "e5m2": (ml_dtypes.float8_e5m2, 14)}[fmt]
    v = np.moveaxis(np.asarray(x, np.float32).astype(ml_dtypes.bfloat16).astype(np.float64), axis, -1)
    blocks = v.reshape(v.shape[:-1] + (-1, 32))
    amax = np.abs(blocks).max(-1, keepdims=True)
    byte = np.maximum(np.where(amax > 0, np.frexp(amax)[1] - 1 + 127, 0) - down, 1)
    scale = np.exp2(byte - 127.0)
    codes = (blocks / scale).astype(np.float32).astype(dtype).astype(np.float64)
    return np.moveaxis((codes * scale).reshape(v.shape), -1, axis)


WIDE = False


def mx_kscale(k):
    if not WIDE:
        return np.ones(k)
    levels = np.array([10, -10, 5, -5, 0])
    a = np.random.permutation(np.resize(levels, k // 512 * 4)).reshape(k // 512, 4)
    idx = np.arange(k)
    return np.exp2(a[idx // 512, idx % 128 // 32])


BF16 = ml_dtypes.bfloat16


def bf(x):
    return np.asarray(x, np.float32).astype(BF16)


def f64(x):
    return np.asarray(x).astype(np.float64)


N, D, H = 128, 512, 1024
LN_EPS = 1e-5
ERF_TERMS = 120


def erf(x):
    a = np.clip(x, -6.0, 6.0)
    term = a
    total = a
    for n in range(1, ERF_TERMS):
        term = term * (2.0 * a * a / (2.0 * n + 1.0))
        total = total + term
    return 2.0 / np.sqrt(np.pi) * np.exp(-a * a) * total


def gelu(v):
    return 0.5 * v * (1.0 + erf(v / np.sqrt(2.0)))


def layernorm(x, g, b):
    m = x.mean(-1, keepdims=True)
    v = np.square(x - m).mean(-1, keepdims=True)
    return (x - m) / np.sqrt(v + LN_EPS) * g + b


def setup_inputs():
    s = mx_kscale(H)
    return {
        "h1": bf(gelu(np.random.standard_normal((N, H))) * s),
        "w2_deq": bf(np.random.standard_normal((H, H)) * 1.5 / np.sqrt(H) / s),
        "b2": bf(0.1 * np.random.standard_normal(H)),
        "g2": bf(1.0 + 0.1 * np.random.standard_normal(H)),
        "b2_ln": bf(0.1 * np.random.standard_normal(H)),
        "Wo": bf(np.random.standard_normal((D, H)) * 1.5 / np.sqrt(H)),
        "bo": bf(0.1 * np.random.standard_normal(D)),
    }


def reference(h1, w2_deq, b2, g2, b2_ln, Wo, bo):
    y = (mxq(f64(h1), 1, "e4m3") @ mxq(f64(w2_deq), 1, "e4m3").T) + f64(b2)
    h2 = gelu(layernorm(y, f64(g2), f64(b2_ln)))
    return (mxq(h2, 1, "e4m3") @ mxq(f64(Wo), 1, "e4m3").T) + f64(bo)

@@ -1,0 +1,204 @@
+from contextlib import ExitStack
+
+import concourse.mybir as mybir
+from concourse.masks import make_identity
+
+F32 = mybir.dt.float32
+BF16 = mybir.dt.bfloat16
+U32 = mybir.dt.uint32
+U8 = mybir.dt.uint8
+FP8X4 = mybir.dt.float8_e4m3fn_x4
+ALU = mybir.AluOpType
+ACT = mybir.ActivationFunctionType
+
+P = 128
+HIDDEN = 1024
+OUT = 512
+K_PASS = 512
+PASSES = HIDDEN // K_PASS
+PACK = 4
+HALVES = 2
+WORDS = K_PASS // 2
+CHUNK = 256
+W2_CHUNKS = HIDDEN // CHUNK
+WO_CHUNKS = OUT // CHUNK
+LN_EPS = 1e-5
+BN_STATS_DIM = 6
+FLOPS = 2 * P * HIDDEN * HIDDEN + 2 * P * HIDDEN * OUT
+
+
+def quantise_rows(nc, stage, grouped_pool, ident_f32, rows_sb, n_rows, codes, scales):
+    words = rows_sb[:].bitcast(F32)
+    grouped = grouped_pool.tile([P, PASSES * n_rows * PACK], BF16, tag="grouped", align_bytes=64)
+    grouped_words = grouped[:].bitcast(F32).rearrange(
+        "p (g r u) -> p g r u", g=PASSES, u=HALVES
+    )
+    for g in range(PASSES):
+        flipped = stage.tile([P, HALVES, n_rows], F32, tag="stage")
+        for u in range(HALVES):
+            first_word = g * WORDS + u * P
+            for b in range(n_rows // P):
+                nc.tensor.transpose(
+                    flipped[:, u, b * P : (b + 1) * P],
+                    words[:, b, first_word : first_word + P],
+                    ident_f32[:],
+                )
+        nc.scalar.copy(out=grouped_words[:, g], in_=flipped[:].rearrange("p u r -> p r u"))
+    nc.vector.quantize_mx(out=codes[:].bitcast(FP8X4), scales=scales[:], in_=grouped[:])
+
+
+def tile_synapsemodel_pb_s_kernel(tc, h1, w2_deq, b2, g2, b2_ln, Wo, bo, out):
+    nc = tc.nc
+    with ExitStack() as ctx:
+        const = ctx.enter_context(tc.tile_pool(name="const", bufs=1))
+        rows_pool = ctx.enter_context(tc.tile_pool(name="rows", bufs=1))
+        grouped_pool = ctx.enter_context(tc.tile_pool(name="grouped", bufs=3))
+        mx = ctx.enter_context(tc.tile_pool(name="mx", bufs=1))
+        work = ctx.enter_context(tc.tile_pool(name="work", bufs=1))
+        stage = ctx.enter_context(tc.psum_pool(name="stage", bufs=4))
+        acc = ctx.enter_context(tc.psum_pool(name="acc", bufs=1))
+
+        h1_sb = rows_pool.tile([P, 1, HIDDEN], BF16, name="h1_sb")
+        nc.sync.dma_start(out=h1_sb[:, 0, :], in_=h1)
+        w2_sb = []
+        for c in range(W2_CHUNKS):
+            w2_c = rows_pool.tile([P, CHUNK // P, HIDDEN], BF16, name="w2_sb%d" % c)
+            nc.sync.dma_start(
+                out=w2_c[:],
+                in_=w2_deq[c * CHUNK : (c + 1) * CHUNK, :].rearrange("(b p) k -> p b k", p=P),
+            )
+            w2_sb.append(w2_c)
+        wo_sb = []
+        for c in range(WO_CHUNKS):
+            wo_c = rows_pool.tile([P, CHUNK // P, HIDDEN], BF16, name="wo_sb%d" % c)
+            nc.sync.dma_start(
+                out=wo_c[:],
+                in_=Wo[c * CHUNK : (c + 1) * CHUNK, :].rearrange("(b p) k -> p b k", p=P),
+            )
+            wo_sb.append(wo_c)
+
+        b2_all = const.tile([P, HIDDEN], BF16, name="b2_all")
+        g2_all = const.tile([P, HIDDEN], BF16, name="g2_all")
+        b2_ln_all = const.tile([P, HIDDEN], BF16, name="b2_ln_all")
+        bo_all = const.tile([P, OUT], BF16, name="bo_all")
+        nc.scalar.dma_start(out=b2_all[:], in_=b2.partition_broadcast(P))
+        nc.scalar.dma_start(out=g2_all[:], in_=g2.partition_broadcast(P))
+        nc.scalar.dma_start(out=b2_ln_all[:], in_=b2_ln.partition_broadcast(P))
+        nc.scalar.dma_start(out=bo_all[:], in_=bo.partition_broadcast(P))
+
+        ident_f32 = const.tile([P, P], F32, name="ident_f32")
+        make_identity(nc, ident_f32[:])
+        ident_bf16 = const.tile([P, P], BF16, name="ident_bf16")
+        make_identity(nc, ident_bf16[:])
+        minus_half = const.tile([P, 1], F32, name="minus_half")
+        nc.gpsimd.memset(minus_half[:], -0.5)
+
+        h1_codes = mx.tile([P, PASSES * P], U32, name="h1_codes", align_bytes=64)
+        h1_scales = mx.tile([P, PASSES * P], U8, name="h1_scales", align_bytes=64)
+        quantise_rows(nc, stage, grouped_pool, ident_f32, h1_sb, P, h1_codes, h1_scales)
+
+        y_biased = work.tile([P, HIDDEN], F32, name="y_biased")
+        stats = work.tile([P, W2_CHUNKS, BN_STATS_DIM], F32, name="stats")
+        for c in range(W2_CHUNKS):
+            w2_codes = mx.tile([P, PASSES * CHUNK], U32, name="w2_codes%d" % c, align_bytes=64)
+            w2_scales = mx.tile([P, PASSES * CHUNK], U8, name="w2_scales%d" % c, align_bytes=64)
+            quantise_rows(nc, stage, grouped_pool, ident_f32, w2_sb[c], CHUNK, w2_codes, w2_scales)
+            first = c * CHUNK
+            y_chunk = acc.tile([P, CHUNK], F32, name="y_chunk%d" % c, tag="acc%d" % c)
+            for g in range(PASSES):
+                nc.tensor.matmul_mx(
+                    out=y_chunk[:],
+                    lhsT=h1_codes[:, g * P : (g + 1) * P].bitcast(FP8X4),
+                    lhsT_scale=h1_scales[:, g * P : (g + 1) * P],
+                    rhs=w2_codes[:, g * CHUNK : (g + 1) * CHUNK].bitcast(FP8X4),
+                    rhs_scale=w2_scales[:, g * CHUNK : (g + 1) * CHUNK],
+                    start=(g == 0),
+                    stop=(g == PASSES - 1),
+                )
+            nc.vector.tensor_tensor(
+                out=y_biased[:, first : first + CHUNK],
+                in0=y_chunk[:],
+                in1=b2_all[:, first : first + CHUNK],
+                op=ALU.add,
+            )
+            nc.vector.bn_stats(out=stats[:, c, :], in_=y_biased[:, first : first + CHUNK])
+
+        wo_codes = []
+        wo_scales = []
+        for c in range(WO_CHUNKS):
+            codes_c = mx.tile([P, PASSES * CHUNK], U32, name="wo_codes%d" % c, align_bytes=64)
+            scales_c = mx.tile([P, PASSES * CHUNK], U8, name="wo_scales%d" % c, align_bytes=64)
+            quantise_rows(nc, stage, grouped_pool, ident_f32, wo_sb[c], CHUNK, codes_c, scales_c)
+            wo_codes.append(codes_c)
+            wo_scales.append(scales_c)
+
+        mean_var = work.tile([P, 2], F32, name="mean_var")
+        nc.vector.bn_aggr(out=mean_var[:], in_=stats[:].rearrange("p c s -> p (c s)"))
+        var_eps = work.tile([P, 1], F32, name="var_eps")
+        rstd = work.tile([P, 1], F32, name="rstd")
+        nc.gpsimd.tensor_scalar(
+            out=var_eps[:], in0=mean_var[:, 1:2], scalar1=LN_EPS, scalar2=None, op0=ALU.add
+        )
+        nc.gpsimd.tensor_tensor(out=rstd[:], in0=var_eps[:], in1=minus_half[:], op=ALU.pow)
+
+        centred = work.tile([P, HIDDEN], F32, name="centred")
+        normed = work.tile([P, HIDDEN], F32, name="normed")
+        h2 = work.tile([P, HIDDEN], BF16, name="h2")
+        h2_by_code = h2[:].rearrange("p (g u q e) -> p g u e q", g=PASSES, u=HALVES, e=2)
+        out_banks = [
+            acc.tile([P, CHUNK], F32, name="out_bank%d" % c, tag="acc%d" % c)
+            for c in range(WO_CHUNKS)
+        ]
+        for g in range(PASSES):
+            cols = slice(g * K_PASS, (g + 1) * K_PASS)
+            nc.vector.scalar_tensor_tensor(
+                out=centred[:, cols],
+                in0=y_biased[:, cols],
+                scalar=mean_var[:, 0:1],
+                in1=g2_all[:, cols],
+                op0=ALU.subtract,
+                op1=ALU.mult,
+            )
+            nc.vector.scalar_tensor_tensor(
+                out=normed[:, cols],
+                in0=centred[:, cols],
+                scalar=rstd[:, 0:1],
+                in1=b2_ln_all[:, cols],
+                op0=ALU.mult,
+                op1=ALU.add,
+            )
+            nc.scalar.activation(out=h2[:, cols], in_=normed[:, cols], func=ACT.Gelu)
+
+            h2_flipped = stage.tile([P, PACK, P], BF16, tag="stage")
+            for u in range(HALVES):
+                for e in range(2):
+                    nc.tensor.transpose(
+                        h2_flipped[:, 2 * u + e, :], h2_by_code[:, g, u, e, :], ident_bf16[:]
+                    )
+            h2_grouped = grouped_pool.tile([P, P, PACK], BF16, tag="h2_grouped", align_bytes=64)
+            nc.vector.tensor_copy(out=h2_grouped[:], in_=h2_flipped[:].rearrange("p t r -> p r t"))
+            h2_codes = mx.tile([P, P], U32, name="h2_codes%d" % g, align_bytes=64)
+            h2_scales = mx.tile([P, P], U8, name="h2_scales%d" % g, align_bytes=64)
+            nc.vector.quantize_mx(
+                out=h2_codes[:].bitcast(FP8X4),
+                scales=h2_scales[:],
+                in_=h2_grouped[:].rearrange("p r t -> p (r t)"),
+            )
+            for c in range(WO_CHUNKS):
+                nc.tensor.matmul_mx(
+                    out=out_banks[c][:],
+                    lhsT=h2_codes[:].bitcast(FP8X4),
+                    lhsT_scale=h2_scales[:],
+                    rhs=wo_codes[c][:, g * CHUNK : (g + 1) * CHUNK].bitcast(FP8X4),
+                    rhs_scale=wo_scales[c][:, g * CHUNK : (g + 1) * CHUNK],
+                    start=(g == 0),
+                    stop=(g == PASSES - 1),
+                )
+
+        out_sb = work.tile([P, OUT], F32, name="out_sb")
+        for c in range(WO_CHUNKS):
+            cols = slice(c * CHUNK, (c + 1) * CHUNK)
+            nc.vector.tensor_tensor(
+                out=out_sb[:, cols], in0=out_banks[c][:], in1=bo_all[:, cols], op=ALU.add
+            )
+        nc.sync.dma_start(out=out, in_=out_sb[:])

@@ -18,33 +18,15 @@ K_PASS = 512
 PASSES = HIDDEN // K_PASS
 PACK = 4
 HALVES = 2
-WORDS = K_PASS // 2
+PAIR = 2
+WORDS = K_PASS // PAIR
 CHUNK = 256
 W2_CHUNKS = HIDDEN // CHUNK
 WO_CHUNKS = OUT // CHUNK
+BANK = 512
 LN_EPS = 1e-5
 BN_STATS_DIM = 6
 FLOPS = 2 * P * HIDDEN * HIDDEN + 2 * P * HIDDEN * OUT
-
-
-def quantise_rows(nc, stage, grouped_pool, ident_f32, rows_sb, n_rows, codes, scales):
-    words = rows_sb[:].bitcast(F32)
-    grouped = grouped_pool.tile([P, PASSES * n_rows * PACK], BF16, tag="grouped", align_bytes=64)
-    grouped_words = grouped[:].bitcast(F32).rearrange(
-        "p (g r u) -> p g r u", g=PASSES, u=HALVES
-    )
-    for g in range(PASSES):
-        flipped = stage.tile([P, HALVES, n_rows], F32, tag="stage")
-        for u in range(HALVES):
-            first_word = g * WORDS + u * P
-            for b in range(n_rows // P):
-                nc.tensor.transpose(
-                    flipped[:, u, b * P : (b + 1) * P],
-                    words[:, b, first_word : first_word + P],
-                    ident_f32[:],
-                )
-        nc.scalar.copy(out=grouped_words[:, g], in_=flipped[:].rearrange("p u r -> p r u"))
-    nc.vector.quantize_mx(out=codes[:].bitcast(FP8X4), scales=scales[:], in_=grouped[:])
 
 
 def tile_synapsemodel_pb_s_kernel(tc, h1, w2_deq, b2, g2, b2_ln, Wo, bo, out):
@@ -57,148 +39,209 @@ def tile_synapsemodel_pb_s_kernel(tc, h1, w2_deq, b2, g2, b2_ln, Wo, bo, out):
         work = ctx.enter_context(tc.tile_pool(name="work", bufs=1))
         stage = ctx.enter_context(tc.psum_pool(name="stage", bufs=4))
         acc = ctx.enter_context(tc.psum_pool(name="acc", bufs=1))
+        ctx.enter_context(tc.manual_schedule())
 
-        h1_sb = rows_pool.tile([P, 1, HIDDEN], BF16, name="h1_sb")
-        nc.sync.dma_start(out=h1_sb[:, 0, :], in_=h1)
-        w2_sb = []
-        for c in range(W2_CHUNKS):
-            w2_c = rows_pool.tile([P, CHUNK // P, HIDDEN], BF16, name="w2_sb%d" % c)
-            nc.sync.dma_start(
-                out=w2_c[:],
-                in_=w2_deq[c * CHUNK : (c + 1) * CHUNK, :].rearrange("(b p) k -> p b k", p=P),
-            )
-            w2_sb.append(w2_c)
-        wo_sb = []
-        for c in range(WO_CHUNKS):
-            wo_c = rows_pool.tile([P, CHUNK // P, HIDDEN], BF16, name="wo_sb%d" % c)
-            nc.sync.dma_start(
-                out=wo_c[:],
-                in_=Wo[c * CHUNK : (c + 1) * CHUNK, :].rearrange("(b p) k -> p b k", p=P),
-            )
-            wo_sb.append(wo_c)
-
-        b2_all = const.tile([P, HIDDEN], BF16, name="b2_all")
-        g2_all = const.tile([P, HIDDEN], BF16, name="g2_all")
-        b2_ln_all = const.tile([P, HIDDEN], BF16, name="b2_ln_all")
-        bo_all = const.tile([P, OUT], BF16, name="bo_all")
-        nc.scalar.dma_start(out=b2_all[:], in_=b2.partition_broadcast(P))
-        nc.scalar.dma_start(out=g2_all[:], in_=g2.partition_broadcast(P))
-        nc.scalar.dma_start(out=b2_ln_all[:], in_=b2_ln.partition_broadcast(P))
-        nc.scalar.dma_start(out=bo_all[:], in_=bo.partition_broadcast(P))
-
+        vec_rows = const.tile([P, PAIR * P], BF16, name="vec_rows")
+        b2_row = const.tile([P, HIDDEN], BF16, name="b2_row")
+        ones = const.tile([P, P], BF16, name="ones")
+        minus_half = const.tile([P, 1], F32, name="minus_half")
+        nc.vector.memset(vec_rows[:], 0.0)
+        nc.vector.memset(b2_row[:], 0.0)
+        nc.vector.memset(ones[:], 1.0)
+        nc.vector.memset(minus_half[:], -0.5)
         ident_f32 = const.tile([P, P], F32, name="ident_f32")
         make_identity(nc, ident_f32[:])
-        ident_bf16 = const.tile([P, P], BF16, name="ident_bf16")
-        make_identity(nc, ident_bf16[:])
-        minus_half = const.tile([P, 1], F32, name="minus_half")
-        nc.gpsimd.memset(minus_half[:], -0.5)
 
-        h1_codes = mx.tile([P, PASSES * P], U32, name="h1_codes", align_bytes=64)
-        h1_scales = mx.tile([P, PASSES * P], U8, name="h1_scales", align_bytes=64)
-        quantise_rows(nc, stage, grouped_pool, ident_f32, h1_sb, P, h1_codes, h1_scales)
+        def load_rows(name, rows, n_rows):
+            rows_sb = rows_pool.tile([P, n_rows // P, HIDDEN], BF16, name=name)
+            nc.sync.dma_start(out=rows_sb[:], in_=rows.rearrange("(b p) k -> p b k", p=P))
+            return rows_sb
 
-        y_biased = work.tile([P, HIDDEN], F32, name="y_biased")
-        stats = work.tile([P, W2_CHUNKS, BN_STATS_DIM], F32, name="stats")
-        for c in range(W2_CHUNKS):
-            w2_codes = mx.tile([P, PASSES * CHUNK], U32, name="w2_codes%d" % c, align_bytes=64)
-            w2_scales = mx.tile([P, PASSES * CHUNK], U8, name="w2_scales%d" % c, align_bytes=64)
-            quantise_rows(nc, stage, grouped_pool, ident_f32, w2_sb[c], CHUNK, w2_codes, w2_scales)
-            first = c * CHUNK
-            y_chunk = acc.tile([P, CHUNK], F32, name="y_chunk%d" % c, tag="acc%d" % c)
-            for g in range(PASSES):
-                nc.tensor.matmul_mx(
-                    out=y_chunk[:],
-                    lhsT=h1_codes[:, g * P : (g + 1) * P].bitcast(FP8X4),
-                    lhsT_scale=h1_scales[:, g * P : (g + 1) * P],
-                    rhs=w2_codes[:, g * CHUNK : (g + 1) * CHUNK].bitcast(FP8X4),
-                    rhs_scale=w2_scales[:, g * CHUNK : (g + 1) * CHUNK],
-                    start=(g == 0),
-                    stop=(g == PASSES - 1),
-                )
-            nc.vector.tensor_tensor(
-                out=y_biased[:, first : first + CHUNK],
-                in0=y_chunk[:],
-                in1=b2_all[:, first : first + CHUNK],
-                op=ALU.add,
-            )
-            nc.vector.bn_stats(out=stats[:, c, :], in_=y_biased[:, first : first + CHUNK])
-
-        wo_codes = []
-        wo_scales = []
-        for c in range(WO_CHUNKS):
-            codes_c = mx.tile([P, PASSES * CHUNK], U32, name="wo_codes%d" % c, align_bytes=64)
-            scales_c = mx.tile([P, PASSES * CHUNK], U8, name="wo_scales%d" % c, align_bytes=64)
-            quantise_rows(nc, stage, grouped_pool, ident_f32, wo_sb[c], CHUNK, codes_c, scales_c)
-            wo_codes.append(codes_c)
-            wo_scales.append(scales_c)
-
-        mean_var = work.tile([P, 2], F32, name="mean_var")
-        nc.vector.bn_aggr(out=mean_var[:], in_=stats[:].rearrange("p c s -> p (c s)"))
-        var_eps = work.tile([P, 1], F32, name="var_eps")
-        rstd = work.tile([P, 1], F32, name="rstd")
-        nc.gpsimd.tensor_scalar(
-            out=var_eps[:], in0=mean_var[:, 1:2], scalar1=LN_EPS, scalar2=None, op0=ALU.add
-        )
-        nc.gpsimd.tensor_tensor(out=rstd[:], in0=var_eps[:], in1=minus_half[:], op=ALU.pow)
-
-        centred = work.tile([P, HIDDEN], F32, name="centred")
-        normed = work.tile([P, HIDDEN], F32, name="normed")
-        h2 = work.tile([P, HIDDEN], BF16, name="h2")
-        h2_by_code = h2[:].rearrange("p (g u q e) -> p g u e q", g=PASSES, u=HALVES, e=2)
-        out_banks = [
-            acc.tile([P, CHUNK], F32, name="out_bank%d" % c, tag="acc%d" % c)
+        h1_sb = load_rows("h1_sb", h1, P)
+        weight_sb = [
+            load_rows("w2_sb%d" % c, w2_deq[c * CHUNK : (c + 1) * CHUNK, :], CHUNK)
+            for c in range(W2_CHUNKS)
+        ] + [
+            load_rows("wo_sb%d" % c, Wo[c * CHUNK : (c + 1) * CHUNK, :], CHUNK)
             for c in range(WO_CHUNKS)
         ]
+        bo_all = const.tile([P, OUT], BF16, name="bo_all")
+        nc.sync.dma_start(out=bo_all[:], in_=bo.partition_broadcast(P))
+
+        nc.scalar.dma_start(out=b2_row[0:1, :], in_=b2.rearrange("(r c) -> r c", r=1))
+        rows_per_vec = HIDDEN // (PAIR * P)
+        nc.scalar.dma_start(
+            out=vec_rows[0:rows_per_vec, :], in_=g2.rearrange("(r c) -> r c", r=rows_per_vec)
+        )
+        nc.scalar.dma_start(
+            out=vec_rows[rows_per_vec : 2 * rows_per_vec, :],
+            in_=b2_ln.rearrange("(r c) -> r c", r=rows_per_vec),
+        )
+        table_warmer = const.tile([P, 1], F32, name="table_warmer")
+        nc.scalar.activation(out=table_warmer[:], in_=minus_half[:], func=ACT.Gelu)
+
+        b2_spread = stage.tile([P, HIDDEN], BF16, tag="stage")
+        for half in range(HIDDEN // BANK):
+            cols = slice(half * BANK, (half + 1) * BANK)
+            nc.tensor.matmul(
+                out=b2_spread[:, cols], lhsT=ones[:], rhs=b2_row[:, cols], start=True, stop=True
+            )
+        b2_all = const.tile([P, HIDDEN], BF16, name="b2_all")
+        nc.scalar.copy(out=b2_all[:], in_=b2_spread[:])
+
+        vec_flipped = stage.tile([P, P], F32, tag="stage")
+        nc.tensor.transpose(vec_flipped[:], vec_rows[:].bitcast(F32), ident_f32[:])
+        affine = const.tile([P, 2 * PASSES * PACK], F32, name="affine")
+        nc.vector.tensor_copy(
+            out=affine[:], in_=vec_flipped[:, 0 : 2 * rows_per_vec].bitcast(BF16)
+        )
+        gain_col = 0
+        shift_col = PASSES * PACK
+
+        def transpose_rows(rows_sb, n_rows):
+            words = rows_sb[:].bitcast(F32)
+            banks = []
+            for g in range(PASSES):
+                flipped = stage.tile([P, HALVES, n_rows], F32, name="flipped%d" % g, tag="stage")
+                for u in range(HALVES):
+                    first_word = g * WORDS + u * P
+                    for b in range(n_rows // P):
+                        nc.tensor.transpose(
+                            flipped[:, u, b * P : (b + 1) * P],
+                            words[:, b, first_word : first_word + P],
+                            ident_f32[:],
+                        )
+                banks.append(flipped)
+            return banks
+
+        def group_rows(banks, n_rows):
+            grouped = grouped_pool.tile(
+                [P, PASSES * n_rows * PACK], BF16, name="grouped", tag="grouped", align_bytes=64
+            )
+            grouped_words = grouped[:].bitcast(F32).rearrange(
+                "p (g r u) -> p g r u", g=PASSES, u=HALVES
+            )
+            for g in range(PASSES):
+                nc.scalar.copy(out=grouped_words[:, g], in_=banks[g][:].rearrange("p u r -> p r u"))
+            return grouped
+
+        def quantise_rows(name, grouped, n_rows):
+            codes = mx.tile([P, PASSES * n_rows], U32, name=name + "_codes", align_bytes=64)
+            scales = mx.tile([P, PASSES * n_rows], U8, name=name + "_scales", align_bytes=64)
+            nc.vector.quantize_mx(out=codes[:].bitcast(FP8X4), scales=scales[:], in_=grouped[:])
+            return codes, scales
+
+        def multiply(acc_tile, left, right, g, right_rows):
+            left_codes, left_scales = left
+            right_codes, right_scales = right
+            nc.tensor.matmul_mx(
+                out=acc_tile[:],
+                lhsT=left_codes[:, g * P : (g + 1) * P].bitcast(FP8X4),
+                lhsT_scale=left_scales[:, g * P : (g + 1) * P],
+                rhs=right_codes[:, g * right_rows : (g + 1) * right_rows].bitcast(FP8X4),
+                rhs_scale=right_scales[:, g * right_rows : (g + 1) * right_rows],
+                start=(g == 0),
+                stop=(g == PASSES - 1),
+            )
+
+        h1_mx = quantise_rows("h1", group_rows(transpose_rows(h1_sb, P), P), P)
+
+        y_biased = work.tile([P, PASSES * PACK, P], F32, name="y_biased")
+        stats = work.tile([P, W2_CHUNKS, BN_STATS_DIM], F32, name="stats")
+
+        def first_product(c, w2_mx):
+            y_chunk = acc.tile([P, CHUNK], F32, name="y_chunk%d" % c, tag="acc%d" % c)
+            for g in range(PASSES):
+                multiply(y_chunk, h1_mx, w2_mx, g, CHUNK)
+            return y_chunk
+
+        def add_bias_and_sum(c, y_chunk):
+            blocks = y_biased[:, PAIR * c : PAIR * (c + 1), :]
+            nc.vector.tensor_tensor(
+                out=blocks,
+                in0=y_chunk[:].rearrange("p (q e) -> p e q", e=PAIR),
+                in1=b2_all[:, c * CHUNK : (c + 1) * CHUNK].rearrange("p (q e) -> p e q", e=PAIR),
+                op=ALU.add,
+            )
+            nc.vector.bn_stats(out=stats[:, c, :], in_=blocks.rearrange("p e q -> p (e q)"))
+
+        mean_var = work.tile([P, 2], F32, name="mean_var")
+        var_eps = work.tile([P, 1], F32, name="var_eps")
+        rstd = work.tile([P, 1], F32, name="rstd")
+
+        def mean_and_rstd():
+            nc.vector.bn_aggr(out=mean_var[:], in_=stats[:].rearrange("p c s -> p (c s)"))
+            nc.vector.tensor_scalar_add(out=var_eps[:], in0=mean_var[:, 1:2], scalar1=LN_EPS)
+            nc.gpsimd.tensor_tensor(out=rstd[:], in0=var_eps[:], in1=minus_half[:], op=ALU.pow)
+
+        n_chunks = W2_CHUNKS + WO_CHUNKS
+        grouped_of = {}
+        weight_mx = {}
+        y_chunk_of = {}
+        for i in range(n_chunks + 1):
+            if i < n_chunks:
+                grouped_of[i] = group_rows(transpose_rows(weight_sb[i], CHUNK), CHUNK)
+            if 1 <= i <= n_chunks:
+                weight_mx[i - 1] = quantise_rows("weight%d" % (i - 1), grouped_of[i - 1], CHUNK)
+                if i - 1 < W2_CHUNKS:
+                    y_chunk_of[i - 1] = first_product(i - 1, weight_mx[i - 1])
+            if 2 <= i < W2_CHUNKS + 2:
+                add_bias_and_sum(i - 2, y_chunk_of[i - 2])
+            if i - 2 == W2_CHUNKS - 1:
+                mean_and_rstd()
+
+        x_hat = work.tile([P, PASSES * PACK, P], F32, name="x_hat")
         for g in range(PASSES):
-            cols = slice(g * K_PASS, (g + 1) * K_PASS)
-            nc.vector.scalar_tensor_tensor(
-                out=centred[:, cols],
-                in0=y_biased[:, cols],
-                scalar=mean_var[:, 0:1],
-                in1=g2_all[:, cols],
+            blocks = slice(g * PACK, (g + 1) * PACK)
+            nc.vector.tensor_scalar(
+                out=x_hat[:, blocks, :],
+                in0=y_biased[:, blocks, :],
+                scalar1=mean_var[:, 0:1],
+                scalar2=rstd[:, 0:1],
                 op0=ALU.subtract,
                 op1=ALU.mult,
             )
-            nc.vector.scalar_tensor_tensor(
-                out=normed[:, cols],
-                in0=centred[:, cols],
-                scalar=rstd[:, 0:1],
-                in1=b2_ln_all[:, cols],
-                op0=ALU.mult,
-                op1=ALU.add,
-            )
-            nc.scalar.activation(out=h2[:, cols], in_=normed[:, cols], func=ACT.Gelu)
 
-            h2_flipped = stage.tile([P, PACK, P], BF16, tag="stage")
-            for u in range(HALVES):
-                for e in range(2):
-                    nc.tensor.transpose(
-                        h2_flipped[:, 2 * u + e, :], h2_by_code[:, g, u, e, :], ident_bf16[:]
-                    )
-            h2_grouped = grouped_pool.tile([P, P, PACK], BF16, tag="h2_grouped", align_bytes=64)
-            nc.vector.tensor_copy(out=h2_grouped[:], in_=h2_flipped[:].rearrange("p t r -> p r t"))
-            h2_codes = mx.tile([P, P], U32, name="h2_codes%d" % g, align_bytes=64)
-            h2_scales = mx.tile([P, P], U8, name="h2_scales%d" % g, align_bytes=64)
+        h2_flipped = [
+            work.tile([P, PACK, P], BF16, name="h2_flipped%d" % g) for g in range(PASSES)
+        ]
+        for g in range(PASSES):
+            for t in range(PACK):
+                x_flipped = stage.tile([P, P], F32, name="x_flipped", tag="stage")
+                nc.tensor.transpose(x_flipped[:], x_hat[:, g * PACK + t, :], ident_f32[:])
+                nc.scalar.activation(
+                    out=h2_flipped[g][:, t, :],
+                    in_=x_flipped[:],
+                    func=ACT.Gelu,
+                    scale=affine[:, gain_col + g * PACK + t : gain_col + g * PACK + t + 1],
+                    bias=affine[:, shift_col + g * PACK + t : shift_col + g * PACK + t + 1],
+                )
+
+        out_chunks = [
+            acc.tile([P, CHUNK], F32, name="out_chunk%d" % c, tag="acc%d" % c)
+            for c in range(WO_CHUNKS)
+        ]
+        h2_codes = mx.tile([P, PASSES * P], U32, name="h2_codes", align_bytes=64)
+        h2_scales = mx.tile([P, PASSES * P], U8, name="h2_scales", align_bytes=64)
+        for g in range(PASSES):
+            h2_grouped = grouped_pool.tile(
+                [P, P, PACK], BF16, name="h2_grouped", tag="h2_grouped", align_bytes=64
+            )
+            nc.vector.tensor_copy(
+                out=h2_grouped[:], in_=h2_flipped[g][:].rearrange("p t r -> p r t")
+            )
             nc.vector.quantize_mx(
-                out=h2_codes[:].bitcast(FP8X4),
-                scales=h2_scales[:],
+                out=h2_codes[:, g * P : (g + 1) * P].bitcast(FP8X4),
+                scales=h2_scales[:, g * P : (g + 1) * P],
                 in_=h2_grouped[:].rearrange("p r t -> p (r t)"),
             )
             for c in range(WO_CHUNKS):
-                nc.tensor.matmul_mx(
-                    out=out_banks[c][:],
-                    lhsT=h2_codes[:].bitcast(FP8X4),
-                    lhsT_scale=h2_scales[:],
-                    rhs=wo_codes[c][:, g * CHUNK : (g + 1) * CHUNK].bitcast(FP8X4),
-                    rhs_scale=wo_scales[c][:, g * CHUNK : (g + 1) * CHUNK],
-                    start=(g == 0),
-                    stop=(g == PASSES - 1),
-                )
+                multiply(out_chunks[c], (h2_codes, h2_scales), weight_mx[W2_CHUNKS + c], g, CHUNK)
 
         out_sb = work.tile([P, OUT], F32, name="out_sb")
         for c in range(WO_CHUNKS):
             cols = slice(c * CHUNK, (c + 1) * CHUNK)
             nc.vector.tensor_tensor(
-                out=out_sb[:, cols], in0=out_banks[c][:], in1=bo_all[:, cols], op=ALU.add
+                out=out_sb[:, cols], in0=out_chunks[c][:], in1=bo_all[:, cols], op=ALU.add
             )
-        nc.sync.dma_start(out=out, in_=out_sb[:])
+            nc.sync.dma_start(out=out[:, cols], in_=out_sb[:, cols])

@@ -19,10 +19,9 @@ PASSES = HIDDEN // K_PASS
 PACK = 4
 HALVES = 2
 PAIR = 2
-WORDS = K_PASS // PAIR
-CHUNK = 256
-W2_CHUNKS = HIDDEN // CHUNK
-WO_CHUNKS = OUT // CHUNK
+W2_CHUNK_ROWS = [256, 256, 256, 128, 128]
+WO_CHUNK_ROWS = [256, 256]
+VEC_ROWS = HIDDEN // (PAIR * P)
 BANK = 512
 LN_EPS = 1e-5
 BN_STATS_DIM = 6
@@ -38,7 +37,7 @@ def tile_synapsemodel_pb_s_kernel(tc, h1, w2_deq, b2, g2, b2_ln, Wo, bo, out):
         mx = ctx.enter_context(tc.tile_pool(name="mx", bufs=1))
         work = ctx.enter_context(tc.tile_pool(name="work", bufs=1))
         stage = ctx.enter_context(tc.psum_pool(name="stage", bufs=4))
-        acc = ctx.enter_context(tc.psum_pool(name="acc", bufs=1))
+        acc = ctx.enter_context(tc.psum_pool(name="acc", bufs=4))
         ctx.enter_context(tc.manual_schedule())
 
         vec_rows = const.tile([P, PAIR * P], BF16, name="vec_rows")
@@ -51,78 +50,82 @@ def tile_synapsemodel_pb_s_kernel(tc, h1, w2_deq, b2, g2, b2_ln, Wo, bo, out):
         nc.vector.memset(minus_half[:], -0.5)
         ident_f32 = const.tile([P, P], F32, name="ident_f32")
         make_identity(nc, ident_f32[:])
-
-        def load_rows(name, rows, n_rows):
-            rows_sb = rows_pool.tile([P, n_rows // P, HIDDEN], BF16, name=name)
-            nc.sync.dma_start(out=rows_sb[:], in_=rows.rearrange("(b p) k -> p b k", p=P))
-            return rows_sb
-
-        h1_sb = load_rows("h1_sb", h1, P)
-        weight_sb = [
-            load_rows("w2_sb%d" % c, w2_deq[c * CHUNK : (c + 1) * CHUNK, :], CHUNK)
-            for c in range(W2_CHUNKS)
-        ] + [
-            load_rows("wo_sb%d" % c, Wo[c * CHUNK : (c + 1) * CHUNK, :], CHUNK)
-            for c in range(WO_CHUNKS)
-        ]
-        bo_all = const.tile([P, OUT], BF16, name="bo_all")
-        nc.sync.dma_start(out=bo_all[:], in_=bo.partition_broadcast(P))
-
-        nc.scalar.dma_start(out=b2_row[0:1, :], in_=b2.rearrange("(r c) -> r c", r=1))
-        rows_per_vec = HIDDEN // (PAIR * P)
-        nc.scalar.dma_start(
-            out=vec_rows[0:rows_per_vec, :], in_=g2.rearrange("(r c) -> r c", r=rows_per_vec)
-        )
-        nc.scalar.dma_start(
-            out=vec_rows[rows_per_vec : 2 * rows_per_vec, :],
-            in_=b2_ln.rearrange("(r c) -> r c", r=rows_per_vec),
-        )
         table_warmer = const.tile([P, 1], F32, name="table_warmer")
         nc.scalar.activation(out=table_warmer[:], in_=minus_half[:], func=ACT.Gelu)
 
-        b2_spread = stage.tile([P, HIDDEN], BF16, tag="stage")
-        for half in range(HIDDEN // BANK):
-            cols = slice(half * BANK, (half + 1) * BANK)
-            nc.tensor.matmul(
-                out=b2_spread[:, cols], lhsT=ones[:], rhs=b2_row[:, cols], start=True, stop=True
-            )
-        b2_all = const.tile([P, HIDDEN], BF16, name="b2_all")
-        nc.scalar.copy(out=b2_all[:], in_=b2_spread[:])
+        def load_chunk(name, rows, n_rows):
+            blocks = []
+            for b in range(n_rows // P):
+                block = rows_pool.tile([P, HIDDEN], BF16, name="%s_%d" % (name, b))
+                nc.sync.dma_start(out=block[:], in_=rows[b * P : (b + 1) * P, :])
+                blocks.append(block)
+            return blocks
 
-        vec_flipped = stage.tile([P, P], F32, tag="stage")
-        nc.tensor.transpose(vec_flipped[:], vec_rows[:].bitcast(F32), ident_f32[:])
+        def load_small_vectors():
+            nc.sync.dma_start(out=b2_row[0:1, :], in_=b2.rearrange("(r c) -> r c", r=1))
+            nc.sync.dma_start(
+                out=vec_rows[0:VEC_ROWS, :], in_=g2.rearrange("(r c) -> r c", r=VEC_ROWS)
+            )
+            nc.sync.dma_start(
+                out=vec_rows[VEC_ROWS : 2 * VEC_ROWS, :],
+                in_=b2_ln.rearrange("(r c) -> r c", r=VEC_ROWS),
+            )
+
+        h1_sb = load_chunk("h1", h1, P)
+        chunk_rows = W2_CHUNK_ROWS + WO_CHUNK_ROWS
+        chunk_first = [sum(W2_CHUNK_ROWS[:c]) for c in range(len(W2_CHUNK_ROWS))] + [
+            sum(WO_CHUNK_ROWS[:c]) for c in range(len(WO_CHUNK_ROWS))
+        ]
+        n_w2 = len(W2_CHUNK_ROWS)
+        n_chunks = len(chunk_rows)
+        chunk_sb = []
+        for i in range(n_chunks):
+            weight = w2_deq if i < n_w2 else Wo
+            rows = weight[chunk_first[i] : chunk_first[i] + chunk_rows[i], :]
+            chunk_sb.append(load_chunk("chunk%d" % i, rows, chunk_rows[i]))
+            if i == 0:
+                load_small_vectors()
+        bo_all = const.tile([P, OUT], BF16, name="bo_all")
+        nc.sync.dma_start(out=bo_all[:], in_=bo.partition_broadcast(P))
+
+        b2_all = const.tile([P, HIDDEN], BF16, name="b2_all")
         affine = const.tile([P, 2 * PASSES * PACK], F32, name="affine")
-        nc.vector.tensor_copy(
-            out=affine[:], in_=vec_flipped[:, 0 : 2 * rows_per_vec].bitcast(BF16)
-        )
         gain_col = 0
         shift_col = PASSES * PACK
 
-        def transpose_rows(rows_sb, n_rows):
-            words = rows_sb[:].bitcast(F32)
-            banks = []
-            for g in range(PASSES):
-                flipped = stage.tile([P, HALVES, n_rows], F32, name="flipped%d" % g, tag="stage")
-                for u in range(HALVES):
-                    first_word = g * WORDS + u * P
-                    for b in range(n_rows // P):
-                        nc.tensor.transpose(
-                            flipped[:, u, b * P : (b + 1) * P],
-                            words[:, b, first_word : first_word + P],
-                            ident_f32[:],
-                        )
-                banks.append(flipped)
-            return banks
+        def spread_small_vectors():
+            b2_spread = stage.tile([P, HIDDEN], BF16, name="b2_spread", tag="stage")
+            for half in range(HIDDEN // BANK):
+                cols = slice(half * BANK, (half + 1) * BANK)
+                nc.tensor.matmul(
+                    out=b2_spread[:, cols], lhsT=ones[:], rhs=b2_row[:, cols], start=True, stop=True
+                )
+            nc.scalar.copy(out=b2_all[:], in_=b2_spread[:])
+            vec_flipped = stage.tile([P, P], F32, name="vec_flipped", tag="stage")
+            nc.tensor.transpose(vec_flipped[:], vec_rows[:].bitcast(F32), ident_f32[:])
+            nc.vector.tensor_copy(out=affine[:], in_=vec_flipped[:, 0 : 2 * VEC_ROWS].bitcast(BF16))
 
-        def group_rows(banks, n_rows):
+        def transpose_and_group(blocks):
+            n_rows = len(blocks) * P
             grouped = grouped_pool.tile(
                 [P, PASSES * n_rows * PACK], BF16, name="grouped", tag="grouped", align_bytes=64
             )
             grouped_words = grouped[:].bitcast(F32).rearrange(
                 "p (g r u) -> p g r u", g=PASSES, u=HALVES
             )
-            for g in range(PASSES):
-                nc.scalar.copy(out=grouped_words[:, g], in_=banks[g][:].rearrange("p u r -> p r u"))
+            for b in range(len(blocks)):
+                words = blocks[b][:].bitcast(F32)
+                flipped = stage.tile([P, PASSES, HALVES, P], F32, name="flipped", tag="stage")
+                for g in range(PASSES):
+                    for u in range(HALVES):
+                        first_word = (g * HALVES + u) * P
+                        nc.tensor.transpose(
+                            flipped[:, g, u, :], words[:, first_word : first_word + P], ident_f32[:]
+                        )
+                nc.scalar.copy(
+                    out=grouped_words[:, :, b * P : (b + 1) * P, :],
+                    in_=flipped[:].rearrange("p g u r -> p g r u"),
+                )
             return grouped
 
         def quantise_rows(name, grouped, n_rows):
@@ -144,52 +147,56 @@ def tile_synapsemodel_pb_s_kernel(tc, h1, w2_deq, b2, g2, b2_ln, Wo, bo, out):
                 stop=(g == PASSES - 1),
             )
 
-        h1_mx = quantise_rows("h1", group_rows(transpose_rows(h1_sb, P), P), P)
+        h1_mx = quantise_rows("h1", transpose_and_group(h1_sb), P)
 
         y_biased = work.tile([P, PASSES * PACK, P], F32, name="y_biased")
-        stats = work.tile([P, W2_CHUNKS, BN_STATS_DIM], F32, name="stats")
-
-        def first_product(c, w2_mx):
-            y_chunk = acc.tile([P, CHUNK], F32, name="y_chunk%d" % c, tag="acc%d" % c)
-            for g in range(PASSES):
-                multiply(y_chunk, h1_mx, w2_mx, g, CHUNK)
-            return y_chunk
-
-        def add_bias_and_sum(c, y_chunk):
-            blocks = y_biased[:, PAIR * c : PAIR * (c + 1), :]
-            nc.vector.tensor_tensor(
-                out=blocks,
-                in0=y_chunk[:].rearrange("p (q e) -> p e q", e=PAIR),
-                in1=b2_all[:, c * CHUNK : (c + 1) * CHUNK].rearrange("p (q e) -> p e q", e=PAIR),
-                op=ALU.add,
-            )
-            nc.vector.bn_stats(out=stats[:, c, :], in_=blocks.rearrange("p e q -> p (e q)"))
-
+        stats = work.tile([P, n_w2, BN_STATS_DIM], F32, name="stats")
         mean_var = work.tile([P, 2], F32, name="mean_var")
         var_eps = work.tile([P, 1], F32, name="var_eps")
         rstd = work.tile([P, 1], F32, name="rstd")
+
+        def first_product(i, w2_mx):
+            y_chunk = acc.tile([P, chunk_rows[i]], F32, name="y_chunk", tag="acc")
+            for g in range(PASSES):
+                multiply(y_chunk, h1_mx, w2_mx, g, chunk_rows[i])
+            return y_chunk
+
+        def add_bias_and_sum(i, y_chunk):
+            first, n_rows = chunk_first[i], chunk_rows[i]
+            first_block = PAIR * (first // (PAIR * P))
+            first_q = (first % (PAIR * P)) // PAIR
+            sorted_cols = y_biased[
+                :, first_block : first_block + PAIR, first_q : first_q + n_rows // PAIR
+            ]
+            nc.vector.tensor_tensor(
+                out=sorted_cols,
+                in0=y_chunk[:].rearrange("p (q e) -> p e q", e=PAIR),
+                in1=b2_all[:, first : first + n_rows].rearrange("p (q e) -> p e q", e=PAIR),
+                op=ALU.add,
+            )
+            nc.vector.bn_stats(out=stats[:, i, :], in_=sorted_cols)
 
         def mean_and_rstd():
             nc.vector.bn_aggr(out=mean_var[:], in_=stats[:].rearrange("p c s -> p (c s)"))
             nc.vector.tensor_scalar_add(out=var_eps[:], in0=mean_var[:, 1:2], scalar1=LN_EPS)
             nc.gpsimd.tensor_tensor(out=rstd[:], in0=var_eps[:], in1=minus_half[:], op=ALU.pow)
 
-        n_chunks = W2_CHUNKS + WO_CHUNKS
         grouped_of = {}
-        weight_mx = {}
+        chunk_mx = {}
         y_chunk_of = {}
-        for i in range(n_chunks + 1):
+        for i in range(max(n_chunks, n_w2 + 2)):
             if i < n_chunks:
-                grouped_of[i] = group_rows(transpose_rows(weight_sb[i], CHUNK), CHUNK)
-            if 1 <= i <= n_chunks:
-                weight_mx[i - 1] = quantise_rows("weight%d" % (i - 1), grouped_of[i - 1], CHUNK)
-                if i - 1 < W2_CHUNKS:
-                    y_chunk_of[i - 1] = first_product(i - 1, weight_mx[i - 1])
-            if 2 <= i < W2_CHUNKS + 2:
+                grouped_of[i] = transpose_and_group(chunk_sb[i])
+            if i == 0:
+                spread_small_vectors()
+            if 1 <= i <= n_w2:
+                chunk_mx[i - 1] = quantise_rows("w2_%d" % (i - 1), grouped_of[i - 1], chunk_rows[i - 1])
+                y_chunk_of[i - 1] = first_product(i - 1, chunk_mx[i - 1])
+            if 2 <= i <= n_w2 + 1:
                 add_bias_and_sum(i - 2, y_chunk_of[i - 2])
-            if i - 2 == W2_CHUNKS - 1:
-                mean_and_rstd()
 
+        mean_and_rstd()
+        chunk_mx[n_w2] = quantise_rows("wo_0", grouped_of[n_w2], chunk_rows[n_w2])
         x_hat = work.tile([P, PASSES * PACK, P], F32, name="x_hat")
         for g in range(PASSES):
             blocks = slice(g * PACK, (g + 1) * PACK)
@@ -201,6 +208,7 @@ def tile_synapsemodel_pb_s_kernel(tc, h1, w2_deq, b2, g2, b2_ln, Wo, bo, out):
                 op0=ALU.subtract,
                 op1=ALU.mult,
             )
+        chunk_mx[n_w2 + 1] = quantise_rows("wo_1", grouped_of[n_w2 + 1], chunk_rows[n_w2 + 1])
 
         h2_flipped = [
             work.tile([P, PACK, P], BF16, name="h2_flipped%d" % g) for g in range(PASSES)
@@ -218,8 +226,8 @@ def tile_synapsemodel_pb_s_kernel(tc, h1, w2_deq, b2, g2, b2_ln, Wo, bo, out):
                 )
 
         out_chunks = [
-            acc.tile([P, CHUNK], F32, name="out_chunk%d" % c, tag="acc%d" % c)
-            for c in range(WO_CHUNKS)
+            acc.tile([P, chunk_rows[i]], F32, name="out_chunk%d" % i, tag="acc")
+            for i in range(n_w2, n_chunks)
         ]
         h2_codes = mx.tile([P, PASSES * P], U32, name="h2_codes", align_bytes=64)
         h2_scales = mx.tile([P, PASSES * P], U8, name="h2_scales", align_bytes=64)
@@ -235,13 +243,13 @@ def tile_synapsemodel_pb_s_kernel(tc, h1, w2_deq, b2, g2, b2_ln, Wo, bo, out):
                 scales=h2_scales[:, g * P : (g + 1) * P],
                 in_=h2_grouped[:].rearrange("p r t -> p (r t)"),
             )
-            for c in range(WO_CHUNKS):
-                multiply(out_chunks[c], (h2_codes, h2_scales), weight_mx[W2_CHUNKS + c], g, CHUNK)
+            for i in range(n_w2, n_chunks):
+                multiply(out_chunks[i - n_w2], (h2_codes, h2_scales), chunk_mx[i], g, chunk_rows[i])
 
         out_sb = work.tile([P, OUT], F32, name="out_sb")
-        for c in range(WO_CHUNKS):
-            cols = slice(c * CHUNK, (c + 1) * CHUNK)
+        for i in range(n_w2, n_chunks):
+            cols = slice(chunk_first[i], chunk_first[i] + chunk_rows[i])
             nc.vector.tensor_tensor(
-                out=out_sb[:, cols], in0=out_chunks[c][:], in1=bo_all[:, cols], op=ALU.add
+                out=out_sb[:, cols], in0=out_chunks[i - n_w2][:], in1=bo_all[:, cols], op=ALU.add
             )
             nc.sync.dma_start(out=out[:, cols], in_=out_sb[:, cols])

@@ -7,6 +7,7 @@ F32 = mybir.dt.float32
 BF16 = mybir.dt.bfloat16
 U32 = mybir.dt.uint32
 U8 = mybir.dt.uint8
+I32 = mybir.dt.int32
 FP8X4 = mybir.dt.float8_e4m3fn_x4
 ALU = mybir.AluOpType
 ACT = mybir.ActivationFunctionType
@@ -23,6 +24,9 @@ W2_CHUNK_ROWS = [256, 256, 256, 128, 128]
 WO_CHUNK_ROWS = [256, 256]
 VEC_ROWS = HIDDEN // (PAIR * P)
 BANK = 512
+IDLE_COLS = 256
+WARM_UP_PASSES = 6
+KEEP_WARM_PASSES = 2
 LN_EPS = 1e-5
 BN_STATS_DIM = 6
 FLOPS = 2 * P * HIDDEN * HIDDEN + 2 * P * HIDDEN * OUT
@@ -37,8 +41,30 @@ def tile_synapsemodel_pb_s_kernel(tc, h1, w2_deq, b2, g2, b2_ln, Wo, bo, out):
         mx = ctx.enter_context(tc.tile_pool(name="mx", bufs=1))
         work = ctx.enter_context(tc.tile_pool(name="work", bufs=1))
         stage = ctx.enter_context(tc.psum_pool(name="stage", bufs=4))
-        acc = ctx.enter_context(tc.psum_pool(name="acc", bufs=4))
+        acc = ctx.enter_context(tc.psum_pool(name="acc", bufs=3))
+        spare = ctx.enter_context(tc.psum_pool(name="spare", bufs=1))
         ctx.enter_context(tc.manual_schedule())
+
+        zeros = const.tile([P, IDLE_COLS * PACK], BF16, name="zeros", align_bytes=64)
+        nc.vector.memset(zeros[:].bitcast(I32), 0)
+        zero_codes = mx.tile([P, IDLE_COLS], U32, name="zero_codes", align_bytes=64)
+        zero_scales = mx.tile([P, IDLE_COLS], U8, name="zero_scales", align_bytes=64)
+        nc.vector.quantize_mx(out=zero_codes[:].bitcast(FP8X4), scales=zero_scales[:], in_=zeros[:])
+        unread = spare.tile([P, IDLE_COLS], F32, name="unread")
+
+        def idle_passes(n_passes):
+            for n in range(n_passes):
+                nc.tensor.matmul_mx(
+                    out=unread[:],
+                    lhsT=zero_codes[:, 0:P].bitcast(FP8X4),
+                    lhsT_scale=zero_scales[:, 0:P],
+                    rhs=zero_codes[:].bitcast(FP8X4),
+                    rhs_scale=zero_scales[:],
+                    start=True,
+                    stop=True,
+                )
+
+        idle_passes(WARM_UP_PASSES)
 
         vec_rows = const.tile([P, PAIR * P], BF16, name="vec_rows")
         b2_row = const.tile([P, HIDDEN], BF16, name="b2_row")
@@ -192,6 +218,8 @@ def tile_synapsemodel_pb_s_kernel(tc, h1, w2_deq, b2, g2, b2_ln, Wo, bo, out):
             if 1 <= i <= n_w2:
                 chunk_mx[i - 1] = quantise_rows("w2_%d" % (i - 1), grouped_of[i - 1], chunk_rows[i - 1])
                 y_chunk_of[i - 1] = first_product(i - 1, chunk_mx[i - 1])
+            if i >= 1:
+                idle_passes(KEEP_WARM_PASSES)
             if 2 <= i <= n_w2 + 1:
                 add_bias_and_sum(i - 2, y_chunk_of[i - 2])
 

@@ -7,7 +7,6 @@ F32 = mybir.dt.float32
 BF16 = mybir.dt.bfloat16
 U32 = mybir.dt.uint32
 U8 = mybir.dt.uint8
-I32 = mybir.dt.int32
 FP8X4 = mybir.dt.float8_e4m3fn_x4
 ALU = mybir.AluOpType
 ACT = mybir.ActivationFunctionType
@@ -20,13 +19,10 @@ PASSES = HIDDEN // K_PASS
 PACK = 4
 HALVES = 2
 PAIR = 2
-W2_CHUNK_ROWS = [256, 256, 256, 128, 128]
-WO_CHUNK_ROWS = [256, 256]
+W2_CHUNK_BLOCKS = [2, 2, 2, 1, 1]
+WO_CHUNK_BLOCKS = [2, 2]
 VEC_ROWS = HIDDEN // (PAIR * P)
 BANK = 512
-IDLE_COLS = 256
-WARM_UP_PASSES = 6
-KEEP_WARM_PASSES = 2
 LN_EPS = 1e-5
 BN_STATS_DIM = 6
 FLOPS = 2 * P * HIDDEN * HIDDEN + 2 * P * HIDDEN * OUT
@@ -41,37 +37,15 @@ def tile_synapsemodel_pb_s_kernel(tc, h1, w2_deq, b2, g2, b2_ln, Wo, bo, out):
         mx = ctx.enter_context(tc.tile_pool(name="mx", bufs=1))
         work = ctx.enter_context(tc.tile_pool(name="work", bufs=1))
         stage = ctx.enter_context(tc.psum_pool(name="stage", bufs=4))
-        acc = ctx.enter_context(tc.psum_pool(name="acc", bufs=3))
-        spare = ctx.enter_context(tc.psum_pool(name="spare", bufs=1))
+        acc = ctx.enter_context(tc.psum_pool(name="acc", bufs=4))
         ctx.enter_context(tc.manual_schedule())
-
-        zeros = const.tile([P, IDLE_COLS * PACK], BF16, name="zeros", align_bytes=64)
-        nc.vector.memset(zeros[:].bitcast(I32), 0)
-        zero_codes = mx.tile([P, IDLE_COLS], U32, name="zero_codes", align_bytes=64)
-        zero_scales = mx.tile([P, IDLE_COLS], U8, name="zero_scales", align_bytes=64)
-        nc.vector.quantize_mx(out=zero_codes[:].bitcast(FP8X4), scales=zero_scales[:], in_=zeros[:])
-        unread = spare.tile([P, IDLE_COLS], F32, name="unread")
-
-        def idle_passes(n_passes):
-            for n in range(n_passes):
-                nc.tensor.matmul_mx(
-                    out=unread[:],
-                    lhsT=zero_codes[:, 0:P].bitcast(FP8X4),
-                    lhsT_scale=zero_scales[:, 0:P],
-                    rhs=zero_codes[:].bitcast(FP8X4),
-                    rhs_scale=zero_scales[:],
-                    start=True,
-                    stop=True,
-                )
-
-        idle_passes(WARM_UP_PASSES)
 
         vec_rows = const.tile([P, PAIR * P], BF16, name="vec_rows")
         b2_row = const.tile([P, HIDDEN], BF16, name="b2_row")
         ones = const.tile([P, P], BF16, name="ones")
         minus_half = const.tile([P, 1], F32, name="minus_half")
-        nc.vector.memset(vec_rows[:], 0.0)
         nc.vector.memset(b2_row[:], 0.0)
+        nc.vector.memset(vec_rows[:], 0.0)
         nc.vector.memset(ones[:], 1.0)
         nc.vector.memset(minus_half[:], -0.5)
         ident_f32 = const.tile([P, P], F32, name="ident_f32")
@@ -79,38 +53,39 @@ def tile_synapsemodel_pb_s_kernel(tc, h1, w2_deq, b2, g2, b2_ln, Wo, bo, out):
         table_warmer = const.tile([P, 1], F32, name="table_warmer")
         nc.scalar.activation(out=table_warmer[:], in_=minus_half[:], func=ACT.Gelu)
 
-        def load_chunk(name, rows, n_rows):
-            blocks = []
-            for b in range(n_rows // P):
-                block = rows_pool.tile([P, HIDDEN], BF16, name="%s_%d" % (name, b))
-                nc.sync.dma_start(out=block[:], in_=rows[b * P : (b + 1) * P, :])
-                blocks.append(block)
-            return blocks
+        w2_blocks = w2_deq.rearrange("(c q e) k -> q c e k", q=P, e=PAIR)
+        wo_blocks = Wo.rearrange("(b p) k -> p b k", p=P)
 
-        def load_small_vectors():
-            nc.sync.dma_start(out=b2_row[0:1, :], in_=b2.rearrange("(r c) -> r c", r=1))
-            nc.sync.dma_start(
-                out=vec_rows[0:VEC_ROWS, :], in_=g2.rearrange("(r c) -> r c", r=VEC_ROWS)
-            )
-            nc.sync.dma_start(
-                out=vec_rows[VEC_ROWS : 2 * VEC_ROWS, :],
-                in_=b2_ln.rearrange("(r c) -> r c", r=VEC_ROWS),
-            )
+        def load_chunk(name, view, n_blocks):
+            chunk = rows_pool.tile([P, n_blocks, HIDDEN], BF16, name=name)
+            nc.sync.dma_start(out=chunk[:], in_=view)
+            return chunk
 
-        h1_sb = load_chunk("h1", h1, P)
-        chunk_rows = W2_CHUNK_ROWS + WO_CHUNK_ROWS
-        chunk_first = [sum(W2_CHUNK_ROWS[:c]) for c in range(len(W2_CHUNK_ROWS))] + [
-            sum(WO_CHUNK_ROWS[:c]) for c in range(len(WO_CHUNK_ROWS))
+        n_w2 = len(W2_CHUNK_BLOCKS)
+        chunk_blocks = W2_CHUNK_BLOCKS + WO_CHUNK_BLOCKS
+        chunk_first = [sum(W2_CHUNK_BLOCKS[:i]) for i in range(n_w2)] + [
+            sum(WO_CHUNK_BLOCKS[:i]) for i in range(len(WO_CHUNK_BLOCKS))
         ]
-        n_w2 = len(W2_CHUNK_ROWS)
-        n_chunks = len(chunk_rows)
+        n_chunks = len(chunk_blocks)
+        h1_sb = load_chunk("h1_sb", h1.rearrange("(b p) k -> p b k", p=P), 1)
         chunk_sb = []
         for i in range(n_chunks):
-            weight = w2_deq if i < n_w2 else Wo
-            rows = weight[chunk_first[i] : chunk_first[i] + chunk_rows[i], :]
-            chunk_sb.append(load_chunk("chunk%d" % i, rows, chunk_rows[i]))
+            first, n_blocks = chunk_first[i], chunk_blocks[i]
+            if i < n_w2:
+                view = w2_blocks[:, first // PAIR, first % PAIR : first % PAIR + n_blocks, :]
+            else:
+                view = wo_blocks[:, first : first + n_blocks, :]
+            chunk_sb.append(load_chunk("chunk%d" % i, view, n_blocks))
             if i == 0:
-                load_small_vectors()
+                nc.sync.dma_start(out=b2_row[0:1, :], in_=b2.rearrange("(r c) -> r c", r=1))
+            if i == n_w2 - 1:
+                nc.sync.dma_start(
+                    out=vec_rows[0:VEC_ROWS, :], in_=g2.rearrange("(r c) -> r c", r=VEC_ROWS)
+                )
+                nc.sync.dma_start(
+                    out=vec_rows[VEC_ROWS : 2 * VEC_ROWS, :],
+                    in_=b2_ln.rearrange("(r c) -> r c", r=VEC_ROWS),
+                )
         bo_all = const.tile([P, OUT], BF16, name="bo_all")
         nc.sync.dma_start(out=bo_all[:], in_=bo.partition_broadcast(P))
 
@@ -119,28 +94,30 @@ def tile_synapsemodel_pb_s_kernel(tc, h1, w2_deq, b2, g2, b2_ln, Wo, bo, out):
         gain_col = 0
         shift_col = PASSES * PACK
 
-        def spread_small_vectors():
+        def spread_b2():
             b2_spread = stage.tile([P, HIDDEN], BF16, name="b2_spread", tag="stage")
             for half in range(HIDDEN // BANK):
                 cols = slice(half * BANK, (half + 1) * BANK)
                 nc.tensor.matmul(
                     out=b2_spread[:, cols], lhsT=ones[:], rhs=b2_row[:, cols], start=True, stop=True
                 )
-            nc.scalar.copy(out=b2_all[:], in_=b2_spread[:])
+            return b2_spread
+
+        def flip_gain_and_shift():
             vec_flipped = stage.tile([P, P], F32, name="vec_flipped", tag="stage")
             nc.tensor.transpose(vec_flipped[:], vec_rows[:].bitcast(F32), ident_f32[:])
-            nc.vector.tensor_copy(out=affine[:], in_=vec_flipped[:, 0 : 2 * VEC_ROWS].bitcast(BF16))
+            return vec_flipped
 
-        def transpose_and_group(blocks):
-            n_rows = len(blocks) * P
+        def transpose_and_group(chunk, n_blocks):
+            n_rows = n_blocks * P
             grouped = grouped_pool.tile(
                 [P, PASSES * n_rows * PACK], BF16, name="grouped", tag="grouped", align_bytes=64
             )
             grouped_words = grouped[:].bitcast(F32).rearrange(
                 "p (g r u) -> p g r u", g=PASSES, u=HALVES
             )
-            for b in range(len(blocks)):
-                words = blocks[b][:].bitcast(F32)
+            for b in range(n_blocks):
+                words = chunk[:, b, :].bitcast(F32)
                 flipped = stage.tile([P, PASSES, HALVES, P], F32, name="flipped", tag="stage")
                 for g in range(PASSES):
                     for u in range(HALVES):
@@ -164,7 +141,7 @@ def tile_synapsemodel_pb_s_kernel(tc, h1, w2_deq, b2, g2, b2_ln, Wo, bo, out):
             left_codes, left_scales = left
             right_codes, right_scales = right
             nc.tensor.matmul_mx(
-                out=acc_tile[:],
+                out=acc_tile[:].rearrange("p b q -> p (b q)"),
                 lhsT=left_codes[:, g * P : (g + 1) * P].bitcast(FP8X4),
                 lhsT_scale=left_scales[:, g * P : (g + 1) * P],
                 rhs=right_codes[:, g * right_rows : (g + 1) * right_rows].bitcast(FP8X4),
@@ -173,7 +150,7 @@ def tile_synapsemodel_pb_s_kernel(tc, h1, w2_deq, b2, g2, b2_ln, Wo, bo, out):
                 stop=(g == PASSES - 1),
             )
 
-        h1_mx = quantise_rows("h1", transpose_and_group(h1_sb), P)
+        h1_mx = quantise_rows("h1", transpose_and_group(h1_sb, 1), P)
 
         y_biased = work.tile([P, PASSES * PACK, P], F32, name="y_biased")
         stats = work.tile([P, n_w2, BN_STATS_DIM], F32, name="stats")
@@ -182,25 +159,23 @@ def tile_synapsemodel_pb_s_kernel(tc, h1, w2_deq, b2, g2, b2_ln, Wo, bo, out):
         rstd = work.tile([P, 1], F32, name="rstd")
 
         def first_product(i, w2_mx):
-            y_chunk = acc.tile([P, chunk_rows[i]], F32, name="y_chunk", tag="acc")
+            y_chunk = acc.tile([P, chunk_blocks[i], P], F32, name="y_chunk", tag="acc")
             for g in range(PASSES):
-                multiply(y_chunk, h1_mx, w2_mx, g, chunk_rows[i])
+                multiply(y_chunk, h1_mx, w2_mx, g, chunk_blocks[i] * P)
             return y_chunk
 
+        b2_by_block = b2_all[:].rearrange("p (c q e) -> p c e q", q=P, e=PAIR)
+
         def add_bias_and_sum(i, y_chunk):
-            first, n_rows = chunk_first[i], chunk_rows[i]
-            first_block = PAIR * (first // (PAIR * P))
-            first_q = (first % (PAIR * P)) // PAIR
-            sorted_cols = y_biased[
-                :, first_block : first_block + PAIR, first_q : first_q + n_rows // PAIR
-            ]
+            first, n_blocks = chunk_first[i], chunk_blocks[i]
+            blocks = y_biased[:, first : first + n_blocks, :]
             nc.vector.tensor_tensor(
-                out=sorted_cols,
-                in0=y_chunk[:].rearrange("p (q e) -> p e q", e=PAIR),
-                in1=b2_all[:, first : first + n_rows].rearrange("p (q e) -> p e q", e=PAIR),
+                out=blocks,
+                in0=y_chunk[:],
+                in1=b2_by_block[:, first // PAIR, first % PAIR : first % PAIR + n_blocks, :],
                 op=ALU.add,
             )
-            nc.vector.bn_stats(out=stats[:, i, :], in_=sorted_cols)
+            nc.vector.bn_stats(out=stats[:, i, :], in_=blocks.rearrange("p b q -> p (b q)"))
 
         def mean_and_rstd():
             nc.vector.bn_aggr(out=mean_var[:], in_=stats[:].rearrange("p c s -> p (c s)"))
@@ -211,32 +186,34 @@ def tile_synapsemodel_pb_s_kernel(tc, h1, w2_deq, b2, g2, b2_ln, Wo, bo, out):
         chunk_mx = {}
         y_chunk_of = {}
         for i in range(max(n_chunks, n_w2 + 2)):
+            if i == n_w2 + 1:
+                vec_flipped = flip_gain_and_shift()
             if i < n_chunks:
-                grouped_of[i] = transpose_and_group(chunk_sb[i])
+                grouped_of[i] = transpose_and_group(chunk_sb[i], chunk_blocks[i])
             if i == 0:
-                spread_small_vectors()
+                b2_spread = spread_b2()
             if 1 <= i <= n_w2:
-                chunk_mx[i - 1] = quantise_rows("w2_%d" % (i - 1), grouped_of[i - 1], chunk_rows[i - 1])
+                chunk_mx[i - 1] = quantise_rows("w2_%d" % (i - 1), grouped_of[i - 1], chunk_blocks[i - 1] * P)
                 y_chunk_of[i - 1] = first_product(i - 1, chunk_mx[i - 1])
-            if i >= 1:
-                idle_passes(KEEP_WARM_PASSES)
+            if i == 1:
+                nc.vector.tensor_copy(out=b2_all[:], in_=b2_spread[:])
             if 2 <= i <= n_w2 + 1:
                 add_bias_and_sum(i - 2, y_chunk_of[i - 2])
 
         mean_and_rstd()
-        chunk_mx[n_w2] = quantise_rows("wo_0", grouped_of[n_w2], chunk_rows[n_w2])
+        chunk_mx[n_w2] = quantise_rows("wo_0", grouped_of[n_w2], chunk_blocks[n_w2] * P)
+        nc.vector.tensor_copy(out=affine[:], in_=vec_flipped[:, 0 : 2 * VEC_ROWS].bitcast(BF16))
         x_hat = work.tile([P, PASSES * PACK, P], F32, name="x_hat")
-        for g in range(PASSES):
-            blocks = slice(g * PACK, (g + 1) * PACK)
+        for j in range(PASSES * PACK):
             nc.vector.tensor_scalar(
-                out=x_hat[:, blocks, :],
-                in0=y_biased[:, blocks, :],
+                out=x_hat[:, j, :],
+                in0=y_biased[:, j, :],
                 scalar1=mean_var[:, 0:1],
                 scalar2=rstd[:, 0:1],
                 op0=ALU.subtract,
                 op1=ALU.mult,
             )
-        chunk_mx[n_w2 + 1] = quantise_rows("wo_1", grouped_of[n_w2 + 1], chunk_rows[n_w2 + 1])
+        chunk_mx[n_w2 + 1] = quantise_rows("wo_1", grouped_of[n_w2 + 1], chunk_blocks[n_w2 + 1] * P)
 
         h2_flipped = [
             work.tile([P, PACK, P], BF16, name="h2_flipped%d" % g) for g in range(PASSES)
@@ -254,7 +231,7 @@ def tile_synapsemodel_pb_s_kernel(tc, h1, w2_deq, b2, g2, b2_ln, Wo, bo, out):
                 )
 
         out_chunks = [
-            acc.tile([P, chunk_rows[i]], F32, name="out_chunk%d" % i, tag="acc")
+            acc.tile([P, chunk_blocks[i], P], F32, name="out_chunk%d" % i, tag="acc")
             for i in range(n_w2, n_chunks)
         ]
         h2_codes = mx.tile([P, PASSES * P], U32, name="h2_codes", align_bytes=64)
@@ -272,12 +249,17 @@ def tile_synapsemodel_pb_s_kernel(tc, h1, w2_deq, b2, g2, b2_ln, Wo, bo, out):
                 in_=h2_grouped[:].rearrange("p r t -> p (r t)"),
             )
             for i in range(n_w2, n_chunks):
-                multiply(out_chunks[i - n_w2], (h2_codes, h2_scales), chunk_mx[i], g, chunk_rows[i])
+                multiply(
+                    out_chunks[i - n_w2], (h2_codes, h2_scales), chunk_mx[i], g, chunk_blocks[i] * P
+                )
 
         out_sb = work.tile([P, OUT], F32, name="out_sb")
         for i in range(n_w2, n_chunks):
-            cols = slice(chunk_first[i], chunk_first[i] + chunk_rows[i])
+            cols = slice(chunk_first[i] * P, (chunk_first[i] + chunk_blocks[i]) * P)
             nc.vector.tensor_tensor(
-                out=out_sb[:, cols], in0=out_chunks[i - n_w2][:], in1=bo_all[:, cols], op=ALU.add
+                out=out_sb[:, cols],
+                in0=out_chunks[i - n_w2][:].rearrange("p b q -> p (b q)"),
+                in1=bo_all[:, cols],
+                op=ALU.add,
             )
             nc.sync.dma_start(out=out[:, cols], in_=out_sb[:, cols])

@@ -19,10 +19,13 @@ PASSES = HIDDEN // K_PASS
 PACK = 4
 HALVES = 2
 PAIR = 2
-W2_CHUNK_BLOCKS = [2, 2, 2, 1, 1]
+W2_BLOCKS = HIDDEN // P
+WO_BLOCKS = OUT // P
+W2_CHUNK_BLOCKS = [1, 1, 2, 2, 1, 1]
 WO_CHUNK_BLOCKS = [2, 2]
+Y_GROUPS = [(0, 1), (2, 3), (4, 5), (6,), (7,)]
+WO_GROUP = 2
 VEC_ROWS = HIDDEN // (PAIR * P)
-BANK = 512
 LN_EPS = 1e-5
 BN_STATS_DIM = 6
 FLOPS = 2 * P * HIDDEN * HIDDEN + 2 * P * HIDDEN * OUT
@@ -33,7 +36,7 @@ def tile_synapsemodel_pb_s_kernel(tc, h1, w2_deq, b2, g2, b2_ln, Wo, bo, out):
     with ExitStack() as ctx:
         const = ctx.enter_context(tc.tile_pool(name="const", bufs=1))
         rows_pool = ctx.enter_context(tc.tile_pool(name="rows", bufs=1))
-        grouped_pool = ctx.enter_context(tc.tile_pool(name="grouped", bufs=3))
+        grouped_pool = ctx.enter_context(tc.tile_pool(name="grouped", bufs=6))
         mx = ctx.enter_context(tc.tile_pool(name="mx", bufs=1))
         work = ctx.enter_context(tc.tile_pool(name="work", bufs=1))
         stage = ctx.enter_context(tc.psum_pool(name="stage", bufs=4))
@@ -41,12 +44,8 @@ def tile_synapsemodel_pb_s_kernel(tc, h1, w2_deq, b2, g2, b2_ln, Wo, bo, out):
         ctx.enter_context(tc.manual_schedule())
 
         vec_rows = const.tile([P, PAIR * P], BF16, name="vec_rows")
-        b2_row = const.tile([P, HIDDEN], BF16, name="b2_row")
-        ones = const.tile([P, P], BF16, name="ones")
         minus_half = const.tile([P, 1], F32, name="minus_half")
-        nc.vector.memset(b2_row[:], 0.0)
         nc.vector.memset(vec_rows[:], 0.0)
-        nc.vector.memset(ones[:], 1.0)
         nc.vector.memset(minus_half[:], -0.5)
         ident_f32 = const.tile([P, P], F32, name="ident_f32")
         make_identity(nc, ident_f32[:])
@@ -61,75 +60,69 @@ def tile_synapsemodel_pb_s_kernel(tc, h1, w2_deq, b2, g2, b2_ln, Wo, bo, out):
             nc.sync.dma_start(out=chunk[:], in_=view)
             return chunk
 
-        n_w2 = len(W2_CHUNK_BLOCKS)
-        chunk_blocks = W2_CHUNK_BLOCKS + WO_CHUNK_BLOCKS
-        chunk_first = [sum(W2_CHUNK_BLOCKS[:i]) for i in range(n_w2)] + [
-            sum(WO_CHUNK_BLOCKS[:i]) for i in range(len(WO_CHUNK_BLOCKS))
-        ]
-        n_chunks = len(chunk_blocks)
         h1_sb = load_chunk("h1_sb", h1.rearrange("(b p) k -> p b k", p=P), 1)
-        chunk_sb = []
-        for i in range(n_chunks):
-            first, n_blocks = chunk_first[i], chunk_blocks[i]
-            if i < n_w2:
-                view = w2_blocks[:, first // PAIR, first % PAIR : first % PAIR + n_blocks, :]
-            else:
-                view = wo_blocks[:, first : first + n_blocks, :]
-            chunk_sb.append(load_chunk("chunk%d" % i, view, n_blocks))
-            if i == 0:
-                nc.sync.dma_start(out=b2_row[0:1, :], in_=b2.rearrange("(r c) -> r c", r=1))
-            if i == n_w2 - 1:
-                nc.sync.dma_start(
-                    out=vec_rows[0:VEC_ROWS, :], in_=g2.rearrange("(r c) -> r c", r=VEC_ROWS)
-                )
-                nc.sync.dma_start(
-                    out=vec_rows[VEC_ROWS : 2 * VEC_ROWS, :],
-                    in_=b2_ln.rearrange("(r c) -> r c", r=VEC_ROWS),
-                )
+        for v, vec in enumerate((b2, g2, b2_ln)):
+            nc.sync.dma_start(
+                out=vec_rows[v * VEC_ROWS : (v + 1) * VEC_ROWS, :],
+                in_=vec.rearrange("(r c) -> r c", r=VEC_ROWS),
+            )
+        w2_rows = []
+        for n_blocks in W2_CHUNK_BLOCKS:
+            first = len(w2_rows)
+            view = w2_blocks[:, first // PAIR, first % PAIR : first % PAIR + n_blocks, :]
+            chunk = load_chunk("w2_chunk%d" % first, view, n_blocks)
+            w2_rows += [chunk[:, b, :] for b in range(n_blocks)]
+        wo_rows = []
+        for n_blocks in WO_CHUNK_BLOCKS:
+            first = len(wo_rows)
+            chunk = load_chunk("wo_chunk%d" % first, wo_blocks[:, first : first + n_blocks, :], n_blocks)
+            wo_rows += [chunk[:, b, :] for b in range(n_blocks)]
         bo_all = const.tile([P, OUT], BF16, name="bo_all")
         nc.sync.dma_start(out=bo_all[:], in_=bo.partition_broadcast(P))
 
         b2_all = const.tile([P, HIDDEN], BF16, name="b2_all")
+        b2_cols = const.tile([P, VEC_ROWS], F32, name="b2_cols")
         affine = const.tile([P, 2 * PASSES * PACK], F32, name="affine")
         gain_col = 0
         shift_col = PASSES * PACK
 
-        def spread_b2():
-            b2_spread = stage.tile([P, HIDDEN], BF16, name="b2_spread", tag="stage")
-            for half in range(HIDDEN // BANK):
-                cols = slice(half * BANK, (half + 1) * BANK)
-                nc.tensor.matmul(
-                    out=b2_spread[:, cols], lhsT=ones[:], rhs=b2_row[:, cols], start=True, stop=True
-                )
-            return b2_spread
-
-        def flip_gain_and_shift():
+        def flip_vectors():
             vec_flipped = stage.tile([P, P], F32, name="vec_flipped", tag="stage")
             nc.tensor.transpose(vec_flipped[:], vec_rows[:].bitcast(F32), ident_f32[:])
-            return vec_flipped
-
-        def transpose_and_group(chunk, n_blocks):
-            n_rows = n_blocks * P
-            grouped = grouped_pool.tile(
-                [P, PASSES * n_rows * PACK], BF16, name="grouped", tag="grouped", align_bytes=64
+            nc.vector.tensor_copy(out=b2_cols[:], in_=vec_flipped[:, 0:VEC_ROWS])
+            nc.vector.tensor_copy(
+                out=affine[:], in_=vec_flipped[:, VEC_ROWS : 3 * VEC_ROWS].bitcast(BF16)
             )
+
+        def spread_b2():
+            b2_spread = stage.tile([P, VEC_ROWS, P], F32, name="b2_spread", tag="stage")
+            for r in range(VEC_ROWS):
+                nc.tensor.transpose(
+                    b2_spread[:, r, :], b2_cols[:, r : r + 1].to_broadcast([P, P]), ident_f32[:]
+                )
+            nc.scalar.copy(out=b2_all[:].bitcast(F32), in_=b2_spread[:].rearrange("p r n -> p (r n)"))
+
+        def new_grouped(n_blocks):
+            return grouped_pool.tile(
+                [P, PASSES * n_blocks * P * PACK], BF16, name="grouped", tag="grouped", align_bytes=64
+            )
+
+        def transpose_and_group(rows, b, grouped):
             grouped_words = grouped[:].bitcast(F32).rearrange(
                 "p (g r u) -> p g r u", g=PASSES, u=HALVES
             )
-            for b in range(n_blocks):
-                words = chunk[:, b, :].bitcast(F32)
-                flipped = stage.tile([P, PASSES, HALVES, P], F32, name="flipped", tag="stage")
-                for g in range(PASSES):
-                    for u in range(HALVES):
-                        first_word = (g * HALVES + u) * P
-                        nc.tensor.transpose(
-                            flipped[:, g, u, :], words[:, first_word : first_word + P], ident_f32[:]
-                        )
-                nc.scalar.copy(
-                    out=grouped_words[:, :, b * P : (b + 1) * P, :],
-                    in_=flipped[:].rearrange("p g u r -> p g r u"),
-                )
-            return grouped
+            words = rows.bitcast(F32)
+            flipped = stage.tile([P, PASSES, HALVES, P], F32, name="flipped", tag="stage")
+            for g in range(PASSES):
+                for u in range(HALVES):
+                    first_word = (g * HALVES + u) * P
+                    nc.tensor.transpose(
+                        flipped[:, g, u, :], words[:, first_word : first_word + P], ident_f32[:]
+                    )
+            nc.scalar.copy(
+                out=grouped_words[:, :, b * P : (b + 1) * P, :],
+                in_=flipped[:].rearrange("p g u r -> p g r u"),
+            )
 
         def quantise_rows(name, grouped, n_rows):
             codes = mx.tile([P, PASSES * n_rows], U32, name=name + "_codes", align_bytes=64)
@@ -141,7 +134,7 @@ def tile_synapsemodel_pb_s_kernel(tc, h1, w2_deq, b2, g2, b2_ln, Wo, bo, out):
             left_codes, left_scales = left
             right_codes, right_scales = right
             nc.tensor.matmul_mx(
-                out=acc_tile[:].rearrange("p b q -> p (b q)"),
+                out=acc_tile.rearrange("p b q -> p (b q)"),
                 lhsT=left_codes[:, g * P : (g + 1) * P].bitcast(FP8X4),
                 lhsT_scale=left_scales[:, g * P : (g + 1) * P],
                 rhs=right_codes[:, g * right_rows : (g + 1) * right_rows].bitcast(FP8X4),
@@ -150,59 +143,88 @@ def tile_synapsemodel_pb_s_kernel(tc, h1, w2_deq, b2, g2, b2_ln, Wo, bo, out):
                 stop=(g == PASSES - 1),
             )
 
-        h1_mx = quantise_rows("h1", transpose_and_group(h1_sb, 1), P)
+        h1_grouped = new_grouped(1)
+        transpose_and_group(h1_sb[:, 0, :], 0, h1_grouped)
+        h1_mx = quantise_rows("h1", h1_grouped, P)
 
         y_biased = work.tile([P, PASSES * PACK, P], F32, name="y_biased")
-        stats = work.tile([P, n_w2, BN_STATS_DIM], F32, name="stats")
+        stats = work.tile([P, len(Y_GROUPS), BN_STATS_DIM], F32, name="stats")
         mean_var = work.tile([P, 2], F32, name="mean_var")
         var_eps = work.tile([P, 1], F32, name="var_eps")
         rstd = work.tile([P, 1], F32, name="rstd")
-
-        def first_product(i, w2_mx):
-            y_chunk = acc.tile([P, chunk_blocks[i], P], F32, name="y_chunk", tag="acc")
-            for g in range(PASSES):
-                multiply(y_chunk, h1_mx, w2_mx, g, chunk_blocks[i] * P)
-            return y_chunk
-
         b2_by_block = b2_all[:].rearrange("p (c q e) -> p c e q", q=P, e=PAIR)
+        group_of = {}
+        for n, blocks in enumerate(Y_GROUPS):
+            for place, block in enumerate(blocks):
+                group_of[block] = (n, place)
+        y_bank = {}
 
-        def add_bias_and_sum(i, y_chunk):
-            first, n_blocks = chunk_first[i], chunk_blocks[i]
-            blocks = y_biased[:, first : first + n_blocks, :]
+        def first_product(block, w2_mx):
+            n, place = group_of[block]
+            if place == 0:
+                y_bank[n] = acc.tile([P, len(Y_GROUPS[n]), P], F32, name="y_bank", tag="acc")
+            for g in range(PASSES):
+                multiply(y_bank[n][:, place : place + 1, :], h1_mx, w2_mx, g, P)
+
+        def add_bias(n):
+            first, n_blocks = Y_GROUPS[n][0], len(Y_GROUPS[n])
             nc.vector.tensor_tensor(
-                out=blocks,
-                in0=y_chunk[:],
+                out=y_biased[:, first : first + n_blocks, :],
+                in0=y_bank[n][:],
                 in1=b2_by_block[:, first // PAIR, first % PAIR : first % PAIR + n_blocks, :],
                 op=ALU.add,
             )
-            nc.vector.bn_stats(out=stats[:, i, :], in_=blocks.rearrange("p b q -> p (b q)"))
+
+        def sum_up(n):
+            first, n_blocks = Y_GROUPS[n][0], len(Y_GROUPS[n])
+            nc.vector.bn_stats(
+                out=stats[:, n, :],
+                in_=y_biased[:, first : first + n_blocks, :].rearrange("p b q -> p (b q)"),
+            )
 
         def mean_and_rstd():
             nc.vector.bn_aggr(out=mean_var[:], in_=stats[:].rearrange("p c s -> p (c s)"))
             nc.vector.tensor_scalar_add(out=var_eps[:], in0=mean_var[:, 1:2], scalar1=LN_EPS)
             nc.gpsimd.tensor_tensor(out=rstd[:], in0=var_eps[:], in1=minus_half[:], op=ALU.pow)
 
+        n_wo_groups = WO_BLOCKS // WO_GROUP
+        wo_grouped = []
+        wo_mx = []
+
+        def prepare_wo_block(b):
+            if b % WO_GROUP == 0:
+                wo_grouped.append(new_grouped(WO_GROUP))
+            transpose_and_group(wo_rows[b], b % WO_GROUP, wo_grouped[b // WO_GROUP])
+
+        def quantise_wo_group(n):
+            wo_mx.append(quantise_rows("wo_%d" % n, wo_grouped[n], WO_GROUP * P))
+
         grouped_of = {}
-        chunk_mx = {}
-        y_chunk_of = {}
-        for i in range(max(n_chunks, n_w2 + 2)):
-            if i == n_w2 + 1:
-                vec_flipped = flip_gain_and_shift()
-            if i < n_chunks:
-                grouped_of[i] = transpose_and_group(chunk_sb[i], chunk_blocks[i])
+        w2_mx = {}
+        for i in range(W2_BLOCKS + 3):
+            if i < W2_BLOCKS:
+                grouped_of[i] = new_grouped(1)
+                transpose_and_group(w2_rows[i], 0, grouped_of[i])
+            if i == W2_BLOCKS:
+                prepare_wo_block(0)
             if i == 0:
-                b2_spread = spread_b2()
-            if 1 <= i <= n_w2:
-                chunk_mx[i - 1] = quantise_rows("w2_%d" % (i - 1), grouped_of[i - 1], chunk_blocks[i - 1] * P)
-                y_chunk_of[i - 1] = first_product(i - 1, chunk_mx[i - 1])
-            if i == 1:
-                nc.vector.tensor_copy(out=b2_all[:], in_=b2_spread[:])
-            if 2 <= i <= n_w2 + 1:
-                add_bias_and_sum(i - 2, y_chunk_of[i - 2])
+                flip_vectors()
+            if i == 2:
+                spread_b2()
+            complete = i - 3 in [blocks[-1] for blocks in Y_GROUPS]
+            if complete:
+                add_bias(group_of[i - 3][0])
+            if 1 <= i <= W2_BLOCKS:
+                w2_mx[i - 1] = quantise_rows("w2_%d" % (i - 1), grouped_of[i - 1], P)
+            if 2 <= i <= W2_BLOCKS + 1:
+                first_product(i - 2, w2_mx[i - 2])
+            if complete:
+                sum_up(group_of[i - 3][0])
+        for b in range(1, WO_BLOCKS):
+            prepare_wo_block(b)
 
         mean_and_rstd()
-        chunk_mx[n_w2] = quantise_rows("wo_0", grouped_of[n_w2], chunk_blocks[n_w2] * P)
-        nc.vector.tensor_copy(out=affine[:], in_=vec_flipped[:, 0 : 2 * VEC_ROWS].bitcast(BF16))
+        quantise_wo_group(0)
         x_hat = work.tile([P, PASSES * PACK, P], F32, name="x_hat")
         for j in range(PASSES * PACK):
             nc.vector.tensor_scalar(
@@ -213,7 +235,7 @@ def tile_synapsemodel_pb_s_kernel(tc, h1, w2_deq, b2, g2, b2_ln, Wo, bo, out):
                 op0=ALU.subtract,
                 op1=ALU.mult,
             )
-        chunk_mx[n_w2 + 1] = quantise_rows("wo_1", grouped_of[n_w2 + 1], chunk_blocks[n_w2 + 1] * P)
+        quantise_wo_group(1)
 
         h2_flipped = [
             work.tile([P, PACK, P], BF16, name="h2_flipped%d" % g) for g in range(PASSES)
@@ -230,9 +252,8 @@ def tile_synapsemodel_pb_s_kernel(tc, h1, w2_deq, b2, g2, b2_ln, Wo, bo, out):
                     bias=affine[:, shift_col + g * PACK + t : shift_col + g * PACK + t + 1],
                 )
 
-        out_chunks = [
-            acc.tile([P, chunk_blocks[i], P], F32, name="out_chunk%d" % i, tag="acc")
-            for i in range(n_w2, n_chunks)
+        out_banks = [
+            acc.tile([P, WO_GROUP, P], F32, name="out_bank%d" % n, tag="acc") for n in range(n_wo_groups)
         ]
         h2_codes = mx.tile([P, PASSES * P], U32, name="h2_codes", align_bytes=64)
         h2_scales = mx.tile([P, PASSES * P], U8, name="h2_scales", align_bytes=64)
@@ -248,17 +269,15 @@ def tile_synapsemodel_pb_s_kernel(tc, h1, w2_deq, b2, g2, b2_ln, Wo, bo, out):
                 scales=h2_scales[:, g * P : (g + 1) * P],
                 in_=h2_grouped[:].rearrange("p r t -> p (r t)"),
             )
-            for i in range(n_w2, n_chunks):
-                multiply(
-                    out_chunks[i - n_w2], (h2_codes, h2_scales), chunk_mx[i], g, chunk_blocks[i] * P
-                )
+            for n in range(n_wo_groups):
+                multiply(out_banks[n][:], (h2_codes, h2_scales), wo_mx[n], g, WO_GROUP * P)
 
         out_sb = work.tile([P, OUT], F32, name="out_sb")
-        for i in range(n_w2, n_chunks):
-            cols = slice(chunk_first[i] * P, (chunk_first[i] + chunk_blocks[i]) * P)
+        for n in range(n_wo_groups):
+            cols = slice(n * WO_GROUP * P, (n + 1) * WO_GROUP * P)
             nc.vector.tensor_tensor(
                 out=out_sb[:, cols],
-                in0=out_chunks[i - n_w2][:].rearrange("p b q -> p (b q)"),
+                in0=out_banks[n][:].rearrange("p b q -> p (b q)"),
                 in1=bo_all[:, cols],
                 op=ALU.add,
             )

@@ -25,6 +25,7 @@ W2_CHUNK_BLOCKS = [1, 1, 2, 2, 1, 1]
 WO_CHUNK_BLOCKS = [2, 2]
 Y_GROUPS = [(0, 1), (2, 3), (4, 5), (6,), (7,)]
 WO_GROUP = 2
+BANK = 512
 VEC_ROWS = HIDDEN // (PAIR * P)
 LN_EPS = 1e-5
 BN_STATS_DIM = 6
@@ -102,6 +103,16 @@ def tile_synapsemodel_pb_s_kernel(tc, h1, w2_deq, b2, g2, b2_ln, Wo, bo, out):
                 )
             nc.scalar.copy(out=b2_all[:].bitcast(F32), in_=b2_spread[:].rearrange("p r n -> p (r n)"))
 
+        def keep_busy(n_cols):
+            idle = acc.tile([P, BANK], F32, name="idle", tag="acc")
+            nc.tensor.matmul(
+                out=idle[:, 0:n_cols],
+                lhsT=minus_half[:].to_broadcast([P, P]),
+                rhs=minus_half[:].to_broadcast([P, n_cols]),
+                start=True,
+                stop=True,
+            )
+
         def new_grouped(n_blocks):
             return grouped_pool.tile(
                 [P, PASSES * n_blocks * P * PACK], BF16, name="grouped", tag="grouped", align_bytes=64
@@ -143,6 +154,7 @@ def tile_synapsemodel_pb_s_kernel(tc, h1, w2_deq, b2, g2, b2_ln, Wo, bo, out):
                 stop=(g == PASSES - 1),
             )
 
+        keep_busy(BANK)
         h1_grouped = new_grouped(1)
         transpose_and_group(h1_sb[:, 0, :], 0, h1_grouped)
         h1_mx = quantise_rows("h1", h1_grouped, P)
@@ -205,6 +217,8 @@ def tile_synapsemodel_pb_s_kernel(tc, h1, w2_deq, b2, g2, b2_ln, Wo, bo, out):
             if i < W2_BLOCKS:
                 grouped_of[i] = new_grouped(1)
                 transpose_and_group(w2_rows[i], 0, grouped_of[i])
+            if i in (0, 1, 2, 3, 5):
+                keep_busy(P)
             if i == W2_BLOCKS:
                 prepare_wo_block(0)
             if i == 0:
@@ -222,6 +236,18 @@ def tile_synapsemodel_pb_s_kernel(tc, h1, w2_deq, b2, g2, b2_ln, Wo, bo, out):
                 sum_up(group_of[i - 3][0])
         for b in range(1, WO_BLOCKS):
             prepare_wo_block(b)
+        for g in range(PASSES):
+            busy = acc.tile([P, PASSES, P], F32, name="busy", tag="acc")
+            h1_codes, h1_scales = h1_mx
+            nc.tensor.matmul_mx(
+                out=busy[:].rearrange("p b q -> p (b q)"),
+                lhsT=h1_codes[:, g * P : (g + 1) * P].bitcast(FP8X4),
+                lhsT_scale=h1_scales[:, g * P : (g + 1) * P],
+                rhs=h1_codes[:].bitcast(FP8X4),
+                rhs_scale=h1_scales[:],
+                start=True,
+                stop=True,
+            )
 
         mean_and_rstd()
         quantise_wo_group(0)

@@ -162,7 +162,6 @@ def tile_synapsemodel_pb_s_kernel(tc, h1, w2_deq, b2, g2, b2_ln, Wo, bo, out):
         y_biased = work.tile([P, PASSES * PACK, P], F32, name="y_biased")
         stats = work.tile([P, len(Y_GROUPS), BN_STATS_DIM], F32, name="stats")
         mean_var = work.tile([P, 2], F32, name="mean_var")
-        var_eps = work.tile([P, 1], F32, name="var_eps")
         rstd = work.tile([P, 1], F32, name="rstd")
         b2_by_block = b2_all[:].rearrange("p (c q e) -> p c e q", q=P, e=PAIR)
         group_of = {}
@@ -196,8 +195,14 @@ def tile_synapsemodel_pb_s_kernel(tc, h1, w2_deq, b2, g2, b2_ln, Wo, bo, out):
 
         def mean_and_rstd():
             nc.vector.bn_aggr(out=mean_var[:], in_=stats[:].rearrange("p c s -> p (c s)"))
-            nc.vector.tensor_scalar_add(out=var_eps[:], in0=mean_var[:, 1:2], scalar1=LN_EPS)
-            nc.gpsimd.tensor_tensor(out=rstd[:], in0=var_eps[:], in1=minus_half[:], op=ALU.pow)
+            nc.gpsimd.tensor_tensor(
+                out=rstd[:], in0=mean_var[:, 1:2], in1=minus_half[:], op=ALU.pow
+            )
+
+        def add_eps():
+            nc.vector.tensor_scalar_add(
+                out=stats[:, 0, 2:3], in0=stats[:, 0, 2:3], scalar1=LN_EPS * HIDDEN
+            )
 
         n_wo_groups = WO_BLOCKS // WO_GROUP
         wo_grouped = []
@@ -211,29 +216,62 @@ def tile_synapsemodel_pb_s_kernel(tc, h1, w2_deq, b2, g2, b2_ln, Wo, bo, out):
         def quantise_wo_group(n):
             wo_mx.append(quantise_rows("wo_%d" % n, wo_grouped[n], WO_GROUP * P))
 
-        grouped_of = {}
+        w2_grouped = {}
         w2_mx = {}
-        for i in range(W2_BLOCKS + 3):
-            if i < W2_BLOCKS:
-                grouped_of[i] = new_grouped(1)
-                transpose_and_group(w2_rows[i], 0, grouped_of[i])
-            if i in (0, 1, 2, 3, 5):
-                keep_busy(P)
-            if i == W2_BLOCKS:
-                prepare_wo_block(0)
-            if i == 0:
-                flip_vectors()
-            if i == 2:
-                spread_b2()
-            complete = i - 3 in [blocks[-1] for blocks in Y_GROUPS]
-            if complete:
-                add_bias(group_of[i - 3][0])
-            if 1 <= i <= W2_BLOCKS:
-                w2_mx[i - 1] = quantise_rows("w2_%d" % (i - 1), grouped_of[i - 1], P)
-            if 2 <= i <= W2_BLOCKS + 1:
-                first_product(i - 2, w2_mx[i - 2])
-            if complete:
-                sum_up(group_of[i - 3][0])
+
+        def transpose_w2(b):
+            w2_grouped[b] = new_grouped(1)
+            transpose_and_group(w2_rows[b], 0, w2_grouped[b])
+
+        def quantise_w2(b):
+            w2_mx[b] = quantise_rows("w2_%d" % b, w2_grouped[b], P)
+
+        def multiply_w2(b):
+            first_product(b, w2_mx[b])
+
+        transpose_w2(0)
+        flip_vectors()
+        transpose_w2(1)
+        keep_busy(P)
+        quantise_w2(0)
+        transpose_w2(2)
+        keep_busy(P)
+        spread_b2()
+        quantise_w2(1)
+        transpose_w2(3)
+        keep_busy(P)
+        quantise_w2(2)
+        multiply_w2(0)
+        multiply_w2(1)
+        transpose_w2(4)
+        transpose_w2(5)
+        add_bias(0)
+        quantise_w2(3)
+        sum_up(0)
+        keep_busy(P)
+        multiply_w2(2)
+        multiply_w2(3)
+        quantise_w2(4)
+        add_eps()
+        transpose_w2(6)
+        transpose_w2(7)
+        add_bias(1)
+        quantise_w2(5)
+        sum_up(1)
+        keep_busy(P)
+        multiply_w2(4)
+        multiply_w2(5)
+        quantise_w2(6)
+        add_bias(2)
+        prepare_wo_block(0)
+        quantise_w2(7)
+        multiply_w2(6)
+        multiply_w2(7)
+        add_bias(3)
+        sum_up(2)
+        add_bias(4)
+        sum_up(3)
+        sum_up(4)
         for b in range(1, WO_BLOCKS):
             prepare_wo_block(b)
         for g in range(PASSES):

@@ -118,7 +118,7 @@ def tile_synapsemodel_pb_s_kernel(tc, h1, w2_deq, b2, g2, b2_ln, Wo, bo, out):
                 [P, PASSES * n_blocks * P * PACK], BF16, name="grouped", tag="grouped", align_bytes=64
             )
 
-        def transpose_and_group(rows, b, grouped):
+        def transpose_and_group(rows, b, grouped, copy=nc.scalar.copy):
             grouped_words = grouped[:].bitcast(F32).rearrange(
                 "p (g r u) -> p g r u", g=PASSES, u=HALVES
             )
@@ -130,7 +130,7 @@ def tile_synapsemodel_pb_s_kernel(tc, h1, w2_deq, b2, g2, b2_ln, Wo, bo, out):
                     nc.tensor.transpose(
                         flipped[:, g, u, :], words[:, first_word : first_word + P], ident_f32[:]
                     )
-            nc.scalar.copy(
+            copy(
                 out=grouped_words[:, :, b * P : (b + 1) * P, :],
                 in_=flipped[:].rearrange("p g u r -> p g r u"),
             )
@@ -208,10 +208,10 @@ def tile_synapsemodel_pb_s_kernel(tc, h1, w2_deq, b2, g2, b2_ln, Wo, bo, out):
         wo_grouped = []
         wo_mx = []
 
-        def prepare_wo_block(b):
+        def prepare_wo_block(b, copy=nc.scalar.copy):
             if b % WO_GROUP == 0:
                 wo_grouped.append(new_grouped(WO_GROUP))
-            transpose_and_group(wo_rows[b], b % WO_GROUP, wo_grouped[b // WO_GROUP])
+            transpose_and_group(wo_rows[b], b % WO_GROUP, wo_grouped[b // WO_GROUP], copy)
 
         def quantise_wo_group(n):
             wo_mx.append(quantise_rows("wo_%d" % n, wo_grouped[n], WO_GROUP * P))
@@ -230,20 +230,20 @@ def tile_synapsemodel_pb_s_kernel(tc, h1, w2_deq, b2, g2, b2_ln, Wo, bo, out):
             first_product(b, w2_mx[b])
 
         transpose_w2(0)
-        flip_vectors()
         transpose_w2(1)
         keep_busy(P)
         quantise_w2(0)
         transpose_w2(2)
         keep_busy(P)
-        spread_b2()
         quantise_w2(1)
         transpose_w2(3)
+        flip_vectors()
         keep_busy(P)
         quantise_w2(2)
         multiply_w2(0)
         multiply_w2(1)
         transpose_w2(4)
+        spread_b2()
         transpose_w2(5)
         add_bias(0)
         quantise_w2(3)
@@ -272,8 +272,10 @@ def tile_synapsemodel_pb_s_kernel(tc, h1, w2_deq, b2, g2, b2_ln, Wo, bo, out):
         add_bias(4)
         sum_up(3)
         sum_up(4)
-        for b in range(1, WO_BLOCKS):
+        for b in range(1, WO_BLOCKS - 1):
             prepare_wo_block(b)
+        mean_and_rstd()
+        prepare_wo_block(WO_BLOCKS - 1, copy=nc.vector.tensor_copy)
         for g in range(PASSES):
             busy = acc.tile([P, PASSES, P], F32, name="busy", tag="acc")
             h1_codes, h1_scales = h1_mx
@@ -287,8 +289,6 @@ def tile_synapsemodel_pb_s_kernel(tc, h1, w2_deq, b2, g2, b2_ln, Wo, bo, out):
                 stop=True,
             )
 
-        mean_and_rstd()
-        quantise_wo_group(0)
         x_hat = work.tile([P, PASSES * PACK, P], F32, name="x_hat")
         for j in range(PASSES * PACK):
             nc.vector.tensor_scalar(
@@ -299,7 +299,7 @@ def tile_synapsemodel_pb_s_kernel(tc, h1, w2_deq, b2, g2, b2_ln, Wo, bo, out):
                 op0=ALU.subtract,
                 op1=ALU.mult,
             )
-        quantise_wo_group(1)
+        quantise_wo_group(0)
 
         h2_flipped = [
             work.tile([P, PACK, P], BF16, name="h2_flipped%d" % g) for g in range(PASSES)
@@ -328,6 +328,8 @@ def tile_synapsemodel_pb_s_kernel(tc, h1, w2_deq, b2, g2, b2_ln, Wo, bo, out):
             nc.vector.tensor_copy(
                 out=h2_grouped[:], in_=h2_flipped[g][:].rearrange("p t r -> p r t")
             )
+            if g == 0:
+                quantise_wo_group(1)
             nc.vector.quantize_mx(
                 out=h2_codes[:, g * P : (g + 1) * P].bitcast(FP8X4),
                 scales=h2_scales[:, g * P : (g + 1) * P],

@@ -41,7 +41,8 @@ def tile_synapsemodel_pb_s_kernel(tc, h1, w2_deq, b2, g2, b2_ln, Wo, bo, out):
         mx = ctx.enter_context(tc.tile_pool(name="mx", bufs=1))
         work = ctx.enter_context(tc.tile_pool(name="work", bufs=1))
         stage = ctx.enter_context(tc.psum_pool(name="stage", bufs=4))
-        acc = ctx.enter_context(tc.psum_pool(name="acc", bufs=4))
+        acc = ctx.enter_context(tc.psum_pool(name="acc", bufs=3))
+        spare = ctx.enter_context(tc.psum_pool(name="spare", bufs=1))
         ctx.enter_context(tc.manual_schedule())
 
         vec_rows = const.tile([P, PAIR * P], BF16, name="vec_rows")
@@ -103,8 +104,9 @@ def tile_synapsemodel_pb_s_kernel(tc, h1, w2_deq, b2, g2, b2_ln, Wo, bo, out):
                 )
             nc.scalar.copy(out=b2_all[:].bitcast(F32), in_=b2_spread[:].rearrange("p r n -> p (r n)"))
 
+        idle = spare.tile([P, BANK], F32, name="idle")
+
         def keep_busy(n_cols):
-            idle = acc.tile([P, BANK], F32, name="idle", tag="acc")
             nc.tensor.matmul(
                 out=idle[:, 0:n_cols],
                 lhsT=minus_half[:].to_broadcast([P, P]),
@@ -158,6 +160,19 @@ def tile_synapsemodel_pb_s_kernel(tc, h1, w2_deq, b2, g2, b2_ln, Wo, bo, out):
         h1_grouped = new_grouped(1)
         transpose_and_group(h1_sb[:, 0, :], 0, h1_grouped)
         h1_mx = quantise_rows("h1", h1_grouped, P)
+
+        def keep_busy_mx(times):
+            h1_codes, h1_scales = h1_mx
+            for k in range(times):
+                nc.tensor.matmul_mx(
+                    out=idle[:, 0 : PASSES * P],
+                    lhsT=h1_codes[:, 0:P].bitcast(FP8X4),
+                    lhsT_scale=h1_scales[:, 0:P],
+                    rhs=h1_codes[:].bitcast(FP8X4),
+                    rhs_scale=h1_scales[:],
+                    start=True,
+                    stop=True,
+                )
 
         y_biased = work.tile([P, PASSES * PACK, P], F32, name="y_biased")
         stats = work.tile([P, len(Y_GROUPS), BN_STATS_DIM], F32, name="stats")
@@ -232,38 +247,42 @@ def tile_synapsemodel_pb_s_kernel(tc, h1, w2_deq, b2, g2, b2_ln, Wo, bo, out):
         transpose_w2(0)
         transpose_w2(1)
         keep_busy(P)
+        flip_vectors()
         quantise_w2(0)
         transpose_w2(2)
         keep_busy(P)
         quantise_w2(1)
         transpose_w2(3)
-        flip_vectors()
+        spread_b2()
         keep_busy(P)
+        keep_busy_mx(2)
         quantise_w2(2)
         multiply_w2(0)
         multiply_w2(1)
         transpose_w2(4)
-        spread_b2()
         transpose_w2(5)
-        add_bias(0)
         quantise_w2(3)
-        sum_up(0)
         keep_busy(P)
+        keep_busy_mx(2)
+        add_bias(0)
         multiply_w2(2)
         multiply_w2(3)
         quantise_w2(4)
-        add_eps()
+        sum_up(0)
         transpose_w2(6)
         transpose_w2(7)
         add_bias(1)
         quantise_w2(5)
         sum_up(1)
+        add_eps()
         keep_busy(P)
+        keep_busy_mx(2)
         multiply_w2(4)
         multiply_w2(5)
         quantise_w2(6)
         add_bias(2)
         prepare_wo_block(0)
+        keep_busy_mx(2)
         quantise_w2(7)
         multiply_w2(6)
         multiply_w2(7)
@@ -276,18 +295,7 @@ def tile_synapsemodel_pb_s_kernel(tc, h1, w2_deq, b2, g2, b2_ln, Wo, bo, out):
             prepare_wo_block(b)
         mean_and_rstd()
         prepare_wo_block(WO_BLOCKS - 1, copy=nc.vector.tensor_copy)
-        for g in range(PASSES):
-            busy = acc.tile([P, PASSES, P], F32, name="busy", tag="acc")
-            h1_codes, h1_scales = h1_mx
-            nc.tensor.matmul_mx(
-                out=busy[:].rearrange("p b q -> p (b q)"),
-                lhsT=h1_codes[:, g * P : (g + 1) * P].bitcast(FP8X4),
-                lhsT_scale=h1_scales[:, g * P : (g + 1) * P],
-                rhs=h1_codes[:].bitcast(FP8X4),
-                rhs_scale=h1_scales[:],
-                start=True,
-                stop=True,
-            )
+        keep_busy_mx(6)
 
         x_hat = work.tile([P, PASSES * PACK, P], F32, name="x_hat")
         for j in range(PASSES * PACK):
@@ -315,6 +323,7 @@ def tile_synapsemodel_pb_s_kernel(tc, h1, w2_deq, b2, g2, b2_ln, Wo, bo, out):
                     scale=affine[:, gain_col + g * PACK + t : gain_col + g * PACK + t + 1],
                     bias=affine[:, shift_col + g * PACK + t : shift_col + g * PACK + t + 1],
                 )
+        keep_busy_mx(2)
 
         out_banks = [
             acc.tile([P, WO_GROUP, P], F32, name="out_bank%d" % n, tag="acc") for n in range(n_wo_groups)
@@ -335,6 +344,8 @@ def tile_synapsemodel_pb_s_kernel(tc, h1, w2_deq, b2, g2, b2_ln, Wo, bo, out):
                 scales=h2_scales[:, g * P : (g + 1) * P],
                 in_=h2_grouped[:].rearrange("p r t -> p (r t)"),
             )
+            if g > 0:
+                keep_busy_mx(2)
             for n in range(n_wo_groups):
                 multiply(out_banks[n][:], (h2_codes, h2_scales), wo_mx[n], g, WO_GROUP * P)
 

@@ -21,9 +21,10 @@ HALVES = 2
 PAIR = 2
 W2_BLOCKS = HIDDEN // P
 WO_BLOCKS = OUT // P
-W2_CHUNK_BLOCKS = [1, 1, 2, 2, 1, 1]
+W2_CHUNK_BLOCKS = [1, 1, 1, 1, 2, 1, 1]
 WO_CHUNK_BLOCKS = [2, 2]
-Y_GROUPS = [(0, 1), (2, 3), (4, 5), (6,), (7,)]
+Y_GROUPS = [(0, 1), (2, 3), (4, 5), (6, 7)]
+X_HAT_SLICES = [slice(0, 1), slice(1, 4), slice(4, 8)]
 WO_GROUP = 2
 BANK = 512
 VEC_ROWS = HIDDEN // (PAIR * P)
@@ -47,8 +48,8 @@ def tile_synapsemodel_pb_s_kernel(tc, h1, w2_deq, b2, g2, b2_ln, Wo, bo, out):
 
         vec_rows = const.tile([P, PAIR * P], BF16, name="vec_rows")
         minus_half = const.tile([P, 1], F32, name="minus_half")
-        nc.vector.memset(vec_rows[:], 0.0)
         nc.vector.memset(minus_half[:], -0.5)
+        nc.vector.memset(vec_rows[:], 0.0)
         ident_f32 = const.tile([P, P], F32, name="ident_f32")
         make_identity(nc, ident_f32[:])
         table_warmer = const.tile([P, 1], F32, name="table_warmer")
@@ -83,7 +84,7 @@ def tile_synapsemodel_pb_s_kernel(tc, h1, w2_deq, b2, g2, b2_ln, Wo, bo, out):
         nc.sync.dma_start(out=bo_all[:], in_=bo.partition_broadcast(P))
 
         b2_all = const.tile([P, HIDDEN], BF16, name="b2_all")
-        b2_cols = const.tile([P, VEC_ROWS], F32, name="b2_cols")
+        vec_cols = const.tile([P, 3 * VEC_ROWS], F32, name="vec_cols")
         affine = const.tile([P, 2 * PASSES * PACK], F32, name="affine")
         gain_col = 0
         shift_col = PASSES * PACK
@@ -91,16 +92,13 @@ def tile_synapsemodel_pb_s_kernel(tc, h1, w2_deq, b2, g2, b2_ln, Wo, bo, out):
         def flip_vectors():
             vec_flipped = stage.tile([P, P], F32, name="vec_flipped", tag="stage")
             nc.tensor.transpose(vec_flipped[:], vec_rows[:].bitcast(F32), ident_f32[:])
-            nc.vector.tensor_copy(out=b2_cols[:], in_=vec_flipped[:, 0:VEC_ROWS])
-            nc.vector.tensor_copy(
-                out=affine[:], in_=vec_flipped[:, VEC_ROWS : 3 * VEC_ROWS].bitcast(BF16)
-            )
+            nc.vector.tensor_copy(out=vec_cols[:], in_=vec_flipped[:, 0 : 3 * VEC_ROWS])
 
         def spread_b2():
             b2_spread = stage.tile([P, VEC_ROWS, P], F32, name="b2_spread", tag="stage")
             for r in range(VEC_ROWS):
                 nc.tensor.transpose(
-                    b2_spread[:, r, :], b2_cols[:, r : r + 1].to_broadcast([P, P]), ident_f32[:]
+                    b2_spread[:, r, :], vec_cols[:, r : r + 1].to_broadcast([P, P]), ident_f32[:]
                 )
             nc.scalar.copy(out=b2_all[:].bitcast(F32), in_=b2_spread[:].rearrange("p r n -> p (r n)"))
 
@@ -251,63 +249,59 @@ def tile_synapsemodel_pb_s_kernel(tc, h1, w2_deq, b2, g2, b2_ln, Wo, bo, out):
         quantise_w2(0)
         transpose_w2(2)
         keep_busy(P)
+        spread_b2()
         quantise_w2(1)
         transpose_w2(3)
-        spread_b2()
         keep_busy(P)
-        keep_busy_mx(2)
         quantise_w2(2)
         multiply_w2(0)
         multiply_w2(1)
         transpose_w2(4)
         transpose_w2(5)
-        quantise_w2(3)
-        keep_busy(P)
-        keep_busy_mx(2)
         add_bias(0)
+        quantise_w2(3)
+        sum_up(0)
+        keep_busy(P)
         multiply_w2(2)
         multiply_w2(3)
         quantise_w2(4)
-        sum_up(0)
         transpose_w2(6)
         transpose_w2(7)
         add_bias(1)
         quantise_w2(5)
         sum_up(1)
-        add_eps()
         keep_busy(P)
-        keep_busy_mx(2)
         multiply_w2(4)
         multiply_w2(5)
         quantise_w2(6)
         add_bias(2)
         prepare_wo_block(0)
-        keep_busy_mx(2)
         quantise_w2(7)
+        sum_up(2)
         multiply_w2(6)
         multiply_w2(7)
+        prepare_wo_block(1)
+        prepare_wo_block(2)
         add_bias(3)
-        sum_up(2)
-        add_bias(4)
+        add_eps()
         sum_up(3)
-        sum_up(4)
-        for b in range(1, WO_BLOCKS - 1):
-            prepare_wo_block(b)
         mean_and_rstd()
+        nc.vector.tensor_copy(out=affine[:], in_=vec_cols[:].bitcast(BF16)[:, PASSES * PACK :])
         prepare_wo_block(WO_BLOCKS - 1, copy=nc.vector.tensor_copy)
-        keep_busy_mx(6)
+        keep_busy_mx(4)
 
         x_hat = work.tile([P, PASSES * PACK, P], F32, name="x_hat")
-        for j in range(PASSES * PACK):
+        for blocks in X_HAT_SLICES:
             nc.vector.tensor_scalar(
-                out=x_hat[:, j, :],
-                in0=y_biased[:, j, :],
+                out=x_hat[:, blocks, :],
+                in0=y_biased[:, blocks, :],
                 scalar1=mean_var[:, 0:1],
                 scalar2=rstd[:, 0:1],
                 op0=ALU.subtract,
                 op1=ALU.mult,
             )
-        quantise_wo_group(0)
+        for n in range(n_wo_groups):
+            quantise_wo_group(n)
 
         h2_flipped = [
             work.tile([P, PACK, P], BF16, name="h2_flipped%d" % g) for g in range(PASSES)
@@ -337,8 +331,6 @@ def tile_synapsemodel_pb_s_kernel(tc, h1, w2_deq, b2, g2, b2_ln, Wo, bo, out):
             nc.vector.tensor_copy(
                 out=h2_grouped[:], in_=h2_flipped[g][:].rearrange("p t r -> p r t")
             )
-            if g == 0:
-                quantise_wo_group(1)
             nc.vector.quantize_mx(
                 out=h2_codes[:, g * P : (g + 1) * P].bitcast(FP8X4),
                 scales=h2_scales[:, g * P : (g + 1) * P],

@@ -46,14 +46,14 @@ def tile_synapsemodel_pb_s_kernel(tc, h1, w2_deq, b2, g2, b2_ln, Wo, bo, out):
         spare = ctx.enter_context(tc.psum_pool(name="spare", bufs=1))
         ctx.enter_context(tc.manual_schedule())
 
-        vec_rows = const.tile([P, PAIR * P], BF16, name="vec_rows")
+        b2_rows = const.tile([P, PAIR * P], BF16, name="b2_rows")
+        affine_rows = const.tile([P, PAIR * P], BF16, name="affine_rows")
         minus_half = const.tile([P, 1], F32, name="minus_half")
         nc.vector.memset(minus_half[:], -0.5)
-        nc.vector.memset(vec_rows[:], 0.0)
+        nc.vector.memset(b2_rows[:].bitcast(U32), 0)
+        nc.vector.memset(affine_rows[:].bitcast(U32), 0)
         ident_f32 = const.tile([P, P], F32, name="ident_f32")
         make_identity(nc, ident_f32[:])
-        table_warmer = const.tile([P, 1], F32, name="table_warmer")
-        nc.scalar.activation(out=table_warmer[:], in_=minus_half[:], func=ACT.Gelu)
 
         w2_blocks = w2_deq.rearrange("(c q e) k -> q c e k", q=P, e=PAIR)
         wo_blocks = Wo.rearrange("(b p) k -> p b k", p=P)
@@ -64,41 +64,47 @@ def tile_synapsemodel_pb_s_kernel(tc, h1, w2_deq, b2, g2, b2_ln, Wo, bo, out):
             return chunk
 
         h1_sb = load_chunk("h1_sb", h1.rearrange("(b p) k -> p b k", p=P), 1)
-        for v, vec in enumerate((b2, g2, b2_ln)):
-            nc.sync.dma_start(
-                out=vec_rows[v * VEC_ROWS : (v + 1) * VEC_ROWS, :],
-                in_=vec.rearrange("(r c) -> r c", r=VEC_ROWS),
-            )
+        nc.scalar.dma_start(out=b2_rows[0:VEC_ROWS, :], in_=b2.rearrange("(r c) -> r c", r=VEC_ROWS))
         w2_rows = []
         for n_blocks in W2_CHUNK_BLOCKS:
             first = len(w2_rows)
             view = w2_blocks[:, first // PAIR, first % PAIR : first % PAIR + n_blocks, :]
             chunk = load_chunk("w2_chunk%d" % first, view, n_blocks)
             w2_rows += [chunk[:, b, :] for b in range(n_blocks)]
+        table_warmer = const.tile([P, 1], F32, name="table_warmer")
+        nc.scalar.activation(out=table_warmer[:], in_=minus_half[:], func=ACT.Gelu)
         wo_rows = []
         for n_blocks in WO_CHUNK_BLOCKS:
             first = len(wo_rows)
             chunk = load_chunk("wo_chunk%d" % first, wo_blocks[:, first : first + n_blocks, :], n_blocks)
             wo_rows += [chunk[:, b, :] for b in range(n_blocks)]
+        for v, vec in enumerate((g2, b2_ln)):
+            nc.sync.dma_start(
+                out=affine_rows[v * VEC_ROWS : (v + 1) * VEC_ROWS, :],
+                in_=vec.rearrange("(r c) -> r c", r=VEC_ROWS),
+            )
         bo_all = const.tile([P, OUT], BF16, name="bo_all")
         nc.sync.dma_start(out=bo_all[:], in_=bo.partition_broadcast(P))
 
         b2_all = const.tile([P, HIDDEN], BF16, name="b2_all")
-        vec_cols = const.tile([P, 3 * VEC_ROWS], F32, name="vec_cols")
+        b2_cols = const.tile([P, VEC_ROWS], F32, name="b2_cols")
         affine = const.tile([P, 2 * PASSES * PACK], F32, name="affine")
         gain_col = 0
         shift_col = PASSES * PACK
 
-        def flip_vectors():
-            vec_flipped = stage.tile([P, P], F32, name="vec_flipped", tag="stage")
-            nc.tensor.transpose(vec_flipped[:], vec_rows[:].bitcast(F32), ident_f32[:])
-            nc.vector.tensor_copy(out=vec_cols[:], in_=vec_flipped[:, 0 : 3 * VEC_ROWS])
+        def flip_vectors(rows):
+            flipped = stage.tile([P, P], F32, name="vec_flipped", tag="stage")
+            nc.tensor.transpose(flipped[:], rows[:].bitcast(F32), ident_f32[:])
+            return flipped
+
+        def flip_b2():
+            nc.vector.tensor_copy(out=b2_cols[:], in_=flip_vectors(b2_rows)[:, 0:VEC_ROWS])
 
         def spread_b2():
             b2_spread = stage.tile([P, VEC_ROWS, P], F32, name="b2_spread", tag="stage")
             for r in range(VEC_ROWS):
                 nc.tensor.transpose(
-                    b2_spread[:, r, :], vec_cols[:, r : r + 1].to_broadcast([P, P]), ident_f32[:]
+                    b2_spread[:, r, :], b2_cols[:, r : r + 1].to_broadcast([P, P]), ident_f32[:]
                 )
             nc.scalar.copy(out=b2_all[:].bitcast(F32), in_=b2_spread[:].rearrange("p r n -> p (r n)"))
 
@@ -232,9 +238,9 @@ def tile_synapsemodel_pb_s_kernel(tc, h1, w2_deq, b2, g2, b2_ln, Wo, bo, out):
         w2_grouped = {}
         w2_mx = {}
 
-        def transpose_w2(b):
+        def transpose_w2(b, copy=nc.scalar.copy):
             w2_grouped[b] = new_grouped(1)
-            transpose_and_group(w2_rows[b], 0, w2_grouped[b])
+            transpose_and_group(w2_rows[b], 0, w2_grouped[b], copy)
 
         def quantise_w2(b):
             w2_mx[b] = quantise_rows("w2_%d" % b, w2_grouped[b], P)
@@ -242,41 +248,41 @@ def tile_synapsemodel_pb_s_kernel(tc, h1, w2_deq, b2, g2, b2_ln, Wo, bo, out):
         def multiply_w2(b):
             first_product(b, w2_mx[b])
 
+        keep_busy(P)
         transpose_w2(0)
         transpose_w2(1)
-        keep_busy(P)
-        flip_vectors()
         quantise_w2(0)
-        transpose_w2(2)
         keep_busy(P)
-        spread_b2()
+        transpose_w2(2)
+        flip_b2()
         quantise_w2(1)
-        transpose_w2(3)
+        transpose_w2(3, copy=nc.vector.tensor_copy)
+        spread_b2()
         keep_busy(P)
         quantise_w2(2)
+        transpose_w2(4)
         multiply_w2(0)
         multiply_w2(1)
-        transpose_w2(4)
-        transpose_w2(5)
-        add_bias(0)
         quantise_w2(3)
+        add_bias(0)
+        quantise_w2(4)
+        transpose_w2(5)
+        transpose_w2(6)
         sum_up(0)
+        quantise_w2(5)
         keep_busy(P)
         multiply_w2(2)
         multiply_w2(3)
-        quantise_w2(4)
-        transpose_w2(6)
-        transpose_w2(7)
         add_bias(1)
-        quantise_w2(5)
+        quantise_w2(6)
+        transpose_w2(7)
+        prepare_wo_block(0)
         sum_up(1)
+        quantise_w2(7)
         keep_busy(P)
         multiply_w2(4)
         multiply_w2(5)
-        quantise_w2(6)
         add_bias(2)
-        prepare_wo_block(0)
-        quantise_w2(7)
         sum_up(2)
         multiply_w2(6)
         multiply_w2(7)
@@ -286,9 +292,12 @@ def tile_synapsemodel_pb_s_kernel(tc, h1, w2_deq, b2, g2, b2_ln, Wo, bo, out):
         add_eps()
         sum_up(3)
         mean_and_rstd()
-        nc.vector.tensor_copy(out=affine[:], in_=vec_cols[:].bitcast(BF16)[:, PASSES * PACK :])
+        affine_flipped = flip_vectors(affine_rows)
         prepare_wo_block(WO_BLOCKS - 1, copy=nc.vector.tensor_copy)
-        keep_busy_mx(4)
+        nc.vector.tensor_copy(
+            out=affine[:], in_=affine_flipped[:].bitcast(BF16)[:, 0 : 2 * PASSES * PACK]
+        )
+        keep_busy_mx(6)
 
         x_hat = work.tile([P, PASSES * PACK, P], F32, name="x_hat")
         for blocks in X_HAT_SLICES:

@@ -52,6 +52,14 @@ def tile_synapsemodel_pb_s_kernel(tc, h1, w2_deq, b2, g2, b2_ln, Wo, bo, out):
         nc.vector.memset(minus_half[:], -0.5)
         nc.vector.memset(b2_rows[:].bitcast(U32), 0)
         nc.vector.memset(affine_rows[:].bitcast(U32), 0)
+        eps_sum = const.tile([P, 1], F32, name="eps_sum")
+        nc.vector.tensor_scalar(
+            out=eps_sum[:],
+            in0=minus_half[:],
+            scalar1=-2 * LN_EPS * HIDDEN,
+            scalar2=None,
+            op0=ALU.mult,
+        )
         ident_f32 = const.tile([P, P], F32, name="ident_f32")
         make_identity(nc, ident_f32[:])
 
@@ -219,8 +227,8 @@ def tile_synapsemodel_pb_s_kernel(tc, h1, w2_deq, b2, g2, b2_ln, Wo, bo, out):
             )
 
         def add_eps():
-            nc.vector.tensor_scalar_add(
-                out=stats[:, 0, 2:3], in0=stats[:, 0, 2:3], scalar1=LN_EPS * HIDDEN
+            nc.scalar.activation(
+                out=stats[:, 0, 2:3], in_=stats[:, 0, 2:3], func=ACT.Identity, bias=eps_sum[:]
             )
 
         n_wo_groups = WO_BLOCKS // WO_GROUP
@@ -261,43 +269,43 @@ def tile_synapsemodel_pb_s_kernel(tc, h1, w2_deq, b2, g2, b2_ln, Wo, bo, out):
         keep_busy(P)
         quantise_w2(2)
         transpose_w2(4)
+        transpose_w2(5)
         multiply_w2(0)
         multiply_w2(1)
         quantise_w2(3)
         add_bias(0)
         quantise_w2(4)
-        transpose_w2(5)
         transpose_w2(6)
         sum_up(0)
         quantise_w2(5)
+        transpose_w2(7)
+        quantise_w2(6)
         keep_busy(P)
         multiply_w2(2)
         multiply_w2(3)
         add_bias(1)
-        quantise_w2(6)
-        transpose_w2(7)
+        quantise_w2(7)
+        add_eps()
         prepare_wo_block(0)
         sum_up(1)
-        quantise_w2(7)
         keep_busy(P)
         multiply_w2(4)
         multiply_w2(5)
-        add_bias(2)
-        sum_up(2)
         multiply_w2(6)
         multiply_w2(7)
+        add_bias(2)
+        add_bias(3)
+        sum_up(2)
+        sum_up(3)
         prepare_wo_block(1)
         prepare_wo_block(2)
-        add_bias(3)
-        add_eps()
-        sum_up(3)
         mean_and_rstd()
         affine_flipped = flip_vectors(affine_rows)
         prepare_wo_block(WO_BLOCKS - 1, copy=nc.vector.tensor_copy)
         nc.vector.tensor_copy(
             out=affine[:], in_=affine_flipped[:].bitcast(BF16)[:, 0 : 2 * PASSES * PACK]
         )
-        keep_busy_mx(6)
+        keep_busy_mx(8)
 
         x_hat = work.tile([P, PASSES * PACK, P], F32, name="x_hat")
         for blocks in X_HAT_SLICES:
@@ -326,28 +334,28 @@ def tile_synapsemodel_pb_s_kernel(tc, h1, w2_deq, b2, g2, b2_ln, Wo, bo, out):
                     scale=affine[:, gain_col + g * PACK + t : gain_col + g * PACK + t + 1],
                     bias=affine[:, shift_col + g * PACK + t : shift_col + g * PACK + t + 1],
                 )
-        keep_busy_mx(2)
+        keep_busy_mx(4)
 
         out_banks = [
             acc.tile([P, WO_GROUP, P], F32, name="out_bank%d" % n, tag="acc") for n in range(n_wo_groups)
         ]
         h2_codes = mx.tile([P, PASSES * P], U32, name="h2_codes", align_bytes=64)
         h2_scales = mx.tile([P, PASSES * P], U8, name="h2_scales", align_bytes=64)
+        h2_grouped = [
+            work.tile([P, P, PACK], BF16, name="h2_grouped%d" % g, align_bytes=64) for g in range(PASSES)
+        ]
         for g in range(PASSES):
-            h2_grouped = grouped_pool.tile(
-                [P, P, PACK], BF16, name="h2_grouped", tag="h2_grouped", align_bytes=64
-            )
             nc.vector.tensor_copy(
-                out=h2_grouped[:], in_=h2_flipped[g][:].rearrange("p t r -> p r t")
+                out=h2_grouped[g][:], in_=h2_flipped[g][:].rearrange("p t r -> p r t")
             )
+        for g in range(PASSES):
             nc.vector.quantize_mx(
                 out=h2_codes[:, g * P : (g + 1) * P].bitcast(FP8X4),
                 scales=h2_scales[:, g * P : (g + 1) * P],
-                in_=h2_grouped[:].rearrange("p r t -> p (r t)"),
+                in_=h2_grouped[g][:].rearrange("p r t -> p (r t)"),
             )
-            if g > 0:
-                keep_busy_mx(2)
-            for n in range(n_wo_groups):
+        for n in range(n_wo_groups):
+            for g in range(PASSES):
                 multiply(out_banks[n][:], (h2_codes, h2_scales), wo_mx[n], g, WO_GROUP * P)
 
         out_sb = work.tile([P, OUT], F32, name="out_sb")

@@ -28,6 +28,7 @@ X_HAT_SLICES = [slice(0, 1), slice(1, 4), slice(4, 8)]
 WO_GROUP = 2
 BANK = 512
 VEC_ROWS = HIDDEN // (PAIR * P)
+RUN = 4
 LN_EPS = 1e-5
 BN_STATS_DIM = 6
 FLOPS = 2 * P * HIDDEN * HIDDEN + 2 * P * HIDDEN * OUT
@@ -258,6 +259,7 @@ def tile_synapsemodel_pb_s_kernel(tc, h1, w2_deq, b2, g2, b2_ln, Wo, bo, out):
 
         keep_busy(P)
         transpose_w2(0)
+        keep_busy(P)
         transpose_w2(1)
         quantise_w2(0)
         keep_busy(P)
@@ -266,7 +268,6 @@ def tile_synapsemodel_pb_s_kernel(tc, h1, w2_deq, b2, g2, b2_ln, Wo, bo, out):
         quantise_w2(1)
         transpose_w2(3, copy=nc.vector.tensor_copy)
         spread_b2()
-        keep_busy(P)
         quantise_w2(2)
         transpose_w2(4)
         transpose_w2(5)
@@ -346,7 +347,8 @@ def tile_synapsemodel_pb_s_kernel(tc, h1, w2_deq, b2, g2, b2_ln, Wo, bo, out):
         ]
         for g in range(PASSES):
             nc.vector.tensor_copy(
-                out=h2_grouped[g][:], in_=h2_flipped[g][:].rearrange("p t r -> p r t")
+                out=h2_grouped[g][:].rearrange("p (c i) t -> p c t i", i=RUN),
+                in_=h2_flipped[g][:].rearrange("p t (c i) -> p c t i", i=RUN),
             )
         for g in range(PASSES):
             nc.vector.quantize_mx(

from contextlib import ExitStack

import concourse.mybir as mybir
from concourse.masks import make_identity

F32 = mybir.dt.float32
BF16 = mybir.dt.bfloat16
U32 = mybir.dt.uint32
U8 = mybir.dt.uint8
FP8X4 = mybir.dt.float8_e4m3fn_x4
ALU = mybir.AluOpType
ACT = mybir.ActivationFunctionType

P = 128
HIDDEN = 1024
OUT = 512
K_PASS = 512
PASSES = HIDDEN // K_PASS
PACK = 4
HALVES = 2
PAIR = 2
W2_BLOCKS = HIDDEN // P
WO_BLOCKS = OUT // P
W2_CHUNK_BLOCKS = [1, 1, 1, 1, 2, 1, 1]
WO_CHUNK_BLOCKS = [2, 2]
Y_GROUPS = [(0, 1), (2, 3), (4, 5), (6, 7)]
X_HAT_SLICES = [slice(0, 1), slice(1, 4), slice(4, 8)]
WO_GROUP = 2
BANK = 512
VEC_ROWS = HIDDEN // (PAIR * P)
RUN = 4
LN_EPS = 1e-5
BN_STATS_DIM = 6
FLOPS = 2 * P * HIDDEN * HIDDEN + 2 * P * HIDDEN * OUT


def tile_synapsemodel_pb_s_kernel(tc, h1, w2_deq, b2, g2, b2_ln, Wo, bo, out):
    nc = tc.nc
    with ExitStack() as ctx:
        const = ctx.enter_context(tc.tile_pool(name="const", bufs=1))
        rows_pool = ctx.enter_context(tc.tile_pool(name="rows", bufs=1))
        grouped_pool = ctx.enter_context(tc.tile_pool(name="grouped", bufs=6))
        mx = ctx.enter_context(tc.tile_pool(name="mx", bufs=1))
        work = ctx.enter_context(tc.tile_pool(name="work", bufs=1))
        stage = ctx.enter_context(tc.psum_pool(name="stage", bufs=4))
        acc = ctx.enter_context(tc.psum_pool(name="acc", bufs=3))
        spare = ctx.enter_context(tc.psum_pool(name="spare", bufs=1))
        ctx.enter_context(tc.manual_schedule())

        b2_rows = const.tile([P, PAIR * P], BF16, name="b2_rows")
        affine_rows = const.tile([P, PAIR * P], BF16, name="affine_rows")
        minus_half = const.tile([P, 1], F32, name="minus_half")
        nc.vector.memset(minus_half[:], -0.5)
        nc.vector.memset(b2_rows[:].bitcast(U32), 0)
        nc.vector.memset(affine_rows[:].bitcast(U32), 0)
        eps_sum = const.tile([P, 1], F32, name="eps_sum")
        nc.vector.tensor_scalar(
            out=eps_sum[:],
            in0=minus_half[:],
            scalar1=-2 * LN_EPS * HIDDEN,
            scalar2=None,
            op0=ALU.mult,
        )
        ident_f32 = const.tile([P, P], F32, name="ident_f32")
        make_identity(nc, ident_f32[:])

        w2_blocks = w2_deq.rearrange("(c q e) k -> q c e k", q=P, e=PAIR)
        wo_blocks = Wo.rearrange("(b p) k -> p b k", p=P)

        def load_chunk(name, view, n_blocks):
            chunk = rows_pool.tile([P, n_blocks, HIDDEN], BF16, name=name)
            nc.sync.dma_start(out=chunk[:], in_=view)
            return chunk

        h1_sb = load_chunk("h1_sb", h1.rearrange("(b p) k -> p b k", p=P), 1)
        nc.scalar.dma_start(out=b2_rows[0:VEC_ROWS, :], in_=b2.rearrange("(r c) -> r c", r=VEC_ROWS))
        w2_rows = []
        for n_blocks in W2_CHUNK_BLOCKS:
            first = len(w2_rows)
            view = w2_blocks[:, first // PAIR, first % PAIR : first % PAIR + n_blocks, :]
            chunk = load_chunk("w2_chunk%d" % first, view, n_blocks)
            w2_rows += [chunk[:, b, :] for b in range(n_blocks)]
        table_warmer = const.tile([P, 1], F32, name="table_warmer")
        nc.scalar.activation(out=table_warmer[:], in_=minus_half[:], func=ACT.Gelu)
        wo_rows = []
        for n_blocks in WO_CHUNK_BLOCKS:
            first = len(wo_rows)
            chunk = load_chunk("wo_chunk%d" % first, wo_blocks[:, first : first + n_blocks, :], n_blocks)
            wo_rows += [chunk[:, b, :] for b in range(n_blocks)]
        for v, vec in enumerate((g2, b2_ln)):
            nc.sync.dma_start(
                out=affine_rows[v * VEC_ROWS : (v + 1) * VEC_ROWS, :],
                in_=vec.rearrange("(r c) -> r c", r=VEC_ROWS),
            )
        bo_all = const.tile([P, OUT], BF16, name="bo_all")
        nc.sync.dma_start(out=bo_all[:], in_=bo.partition_broadcast(P))

        b2_all = const.tile([P, HIDDEN], BF16, name="b2_all")
        b2_cols = const.tile([P, VEC_ROWS], F32, name="b2_cols")
        affine = const.tile([P, 2 * PASSES * PACK], F32, name="affine")
        gain_col = 0
        shift_col = PASSES * PACK

        def flip_vectors(rows):
            flipped = stage.tile([P, P], F32, name="vec_flipped", tag="stage")
            nc.tensor.transpose(flipped[:], rows[:].bitcast(F32), ident_f32[:])
            return flipped

        def flip_b2():
            nc.vector.tensor_copy(out=b2_cols[:], in_=flip_vectors(b2_rows)[:, 0:VEC_ROWS])

        def spread_b2():
            b2_spread = stage.tile([P, VEC_ROWS, P], F32, name="b2_spread", tag="stage")
            for r in range(VEC_ROWS):
                nc.tensor.transpose(
                    b2_spread[:, r, :], b2_cols[:, r : r + 1].to_broadcast([P, P]), ident_f32[:]
                )
            nc.scalar.copy(out=b2_all[:].bitcast(F32), in_=b2_spread[:].rearrange("p r n -> p (r n)"))

        idle = spare.tile([P, BANK], F32, name="idle")

        def keep_busy(n_cols):
            nc.tensor.matmul(
                out=idle[:, 0:n_cols],
                lhsT=minus_half[:].to_broadcast([P, P]),
                rhs=minus_half[:].to_broadcast([P, n_cols]),
                start=True,
                stop=True,
            )

        def new_grouped(n_blocks):
            return grouped_pool.tile(
                [P, PASSES * n_blocks * P * PACK], BF16, name="grouped", tag="grouped", align_bytes=64
            )

        def transpose_and_group(rows, b, grouped, copy=nc.scalar.copy):
            grouped_words = grouped[:].bitcast(F32).rearrange(
                "p (g r u) -> p g r u", g=PASSES, u=HALVES
            )
            words = rows.bitcast(F32)
            flipped = stage.tile([P, PASSES, HALVES, P], F32, name="flipped", tag="stage")
            for g in range(PASSES):
                for u in range(HALVES):
                    first_word = (g * HALVES + u) * P
                    nc.tensor.transpose(
                        flipped[:, g, u, :], words[:, first_word : first_word + P], ident_f32[:]
                    )
            copy(
                out=grouped_words[:, :, b * P : (b + 1) * P, :],
                in_=flipped[:].rearrange("p g u r -> p g r u"),
            )

        def quantise_rows(name, grouped, n_rows):
            codes = mx.tile([P, PASSES * n_rows], U32, name=name + "_codes", align_bytes=64)
            scales = mx.tile([P, PASSES * n_rows], U8, name=name + "_scales", align_bytes=64)
            nc.vector.quantize_mx(out=codes[:].bitcast(FP8X4), scales=scales[:], in_=grouped[:])
            return codes, scales

        def multiply(acc_tile, left, right, g, right_rows):
            left_codes, left_scales = left
            right_codes, right_scales = right
            nc.tensor.matmul_mx(
                out=acc_tile.rearrange("p b q -> p (b q)"),
                lhsT=left_codes[:, g * P : (g + 1) * P].bitcast(FP8X4),
                lhsT_scale=left_scales[:, g * P : (g + 1) * P],
                rhs=right_codes[:, g * right_rows : (g + 1) * right_rows].bitcast(FP8X4),
                rhs_scale=right_scales[:, g * right_rows : (g + 1) * right_rows],
                start=(g == 0),
                stop=(g == PASSES - 1),
            )

        keep_busy(BANK)
        h1_grouped = new_grouped(1)
        transpose_and_group(h1_sb[:, 0, :], 0, h1_grouped)
        h1_mx = quantise_rows("h1", h1_grouped, P)

        def keep_busy_mx(times):
            h1_codes, h1_scales = h1_mx
            for k in range(times):
                nc.tensor.matmul_mx(
                    out=idle[:, 0 : PASSES * P],
                    lhsT=h1_codes[:, 0:P].bitcast(FP8X4),
                    lhsT_scale=h1_scales[:, 0:P],
                    rhs=h1_codes[:].bitcast(FP8X4),
                    rhs_scale=h1_scales[:],
                    start=True,
                    stop=True,
                )

        y_biased = work.tile([P, PASSES * PACK, P], F32, name="y_biased")
        stats = work.tile([P, len(Y_GROUPS), BN_STATS_DIM], F32, name="stats")
        mean_var = work.tile([P, 2], F32, name="mean_var")
        rstd = work.tile([P, 1], F32, name="rstd")
        b2_by_block = b2_all[:].rearrange("p (c q e) -> p c e q", q=P, e=PAIR)
        group_of = {}
        for n, blocks in enumerate(Y_GROUPS):
            for place, block in enumerate(blocks):
                group_of[block] = (n, place)
        y_bank = {}

        def first_product(block, w2_mx):
            n, place = group_of[block]
            if place == 0:
                y_bank[n] = acc.tile([P, len(Y_GROUPS[n]), P], F32, name="y_bank", tag="acc")
            for g in range(PASSES):
                multiply(y_bank[n][:, place : place + 1, :], h1_mx, w2_mx, g, P)

        def add_bias(n):
            first, n_blocks = Y_GROUPS[n][0], len(Y_GROUPS[n])
            nc.vector.tensor_tensor(
                out=y_biased[:, first : first + n_blocks, :],
                in0=y_bank[n][:],
                in1=b2_by_block[:, first // PAIR, first % PAIR : first % PAIR + n_blocks, :],
                op=ALU.add,
            )

        def sum_up(n):
            first, n_blocks = Y_GROUPS[n][0], len(Y_GROUPS[n])
            nc.vector.bn_stats(
                out=stats[:, n, :],
                in_=y_biased[:, first : first + n_blocks, :].rearrange("p b q -> p (b q)"),
            )

        def mean_and_rstd():
            nc.vector.bn_aggr(out=mean_var[:], in_=stats[:].rearrange("p c s -> p (c s)"))
            nc.gpsimd.tensor_tensor(
                out=rstd[:], in0=mean_var[:, 1:2], in1=minus_half[:], op=ALU.pow
            )

        def add_eps():
            nc.scalar.activation(
                out=stats[:, 0, 2:3], in_=stats[:, 0, 2:3], func=ACT.Identity, bias=eps_sum[:]
            )

        n_wo_groups = WO_BLOCKS // WO_GROUP
        wo_grouped = []
        wo_mx = []

        def prepare_wo_block(b, copy=nc.scalar.copy):
            if b % WO_GROUP == 0:
                wo_grouped.append(new_grouped(WO_GROUP))
            transpose_and_group(wo_rows[b], b % WO_GROUP, wo_grouped[b // WO_GROUP], copy)

        def quantise_wo_group(n):
            wo_mx.append(quantise_rows("wo_%d" % n, wo_grouped[n], WO_GROUP * P))

        w2_grouped = {}
        w2_mx = {}

        def transpose_w2(b, copy=nc.scalar.copy):
            w2_grouped[b] = new_grouped(1)
            transpose_and_group(w2_rows[b], 0, w2_grouped[b], copy)

        def quantise_w2(b):
            w2_mx[b] = quantise_rows("w2_%d" % b, w2_grouped[b], P)

        def multiply_w2(b):
            first_product(b, w2_mx[b])

        keep_busy(P)
        transpose_w2(0)
        keep_busy(P)
        transpose_w2(1)
        quantise_w2(0)
        keep_busy(P)
        transpose_w2(2)
        flip_b2()
        quantise_w2(1)
        transpose_w2(3, copy=nc.vector.tensor_copy)
        spread_b2()
        quantise_w2(2)
        transpose_w2(4)
        transpose_w2(5)
        multiply_w2(0)
        multiply_w2(1)
        quantise_w2(3)
        add_bias(0)
        quantise_w2(4)
        transpose_w2(6)
        sum_up(0)
        quantise_w2(5)
        transpose_w2(7)
        quantise_w2(6)
        keep_busy(P)
        multiply_w2(2)
        multiply_w2(3)
        add_bias(1)
        quantise_w2(7)
        add_eps()
        prepare_wo_block(0)
        sum_up(1)
        keep_busy(P)
        multiply_w2(4)
        multiply_w2(5)
        multiply_w2(6)
        multiply_w2(7)
        add_bias(2)
        add_bias(3)
        sum_up(2)
        sum_up(3)
        prepare_wo_block(1)
        prepare_wo_block(2)
        mean_and_rstd()
        affine_flipped = flip_vectors(affine_rows)
        prepare_wo_block(WO_BLOCKS - 1, copy=nc.vector.tensor_copy)
        nc.vector.tensor_copy(
            out=affine[:], in_=affine_flipped[:].bitcast(BF16)[:, 0 : 2 * PASSES * PACK]
        )
        keep_busy_mx(8)

        x_hat = work.tile([P, PASSES * PACK, P], F32, name="x_hat")
        for blocks in X_HAT_SLICES:
            nc.vector.tensor_scalar(
                out=x_hat[:, blocks, :],
                in0=y_biased[:, blocks, :],
                scalar1=mean_var[:, 0:1],
                scalar2=rstd[:, 0:1],
                op0=ALU.subtract,
                op1=ALU.mult,
            )
        for n in range(n_wo_groups):
            quantise_wo_group(n)

        h2_flipped = [
            work.tile([P, PACK, P], BF16, name="h2_flipped%d" % g) for g in range(PASSES)
        ]
        for g in range(PASSES):
            for t in range(PACK):
                x_flipped = stage.tile([P, P], F32, name="x_flipped", tag="stage")
                nc.tensor.transpose(x_flipped[:], x_hat[:, g * PACK + t, :], ident_f32[:])
                nc.scalar.activation(
                    out=h2_flipped[g][:, t, :],
                    in_=x_flipped[:],
                    func=ACT.Gelu,
                    scale=affine[:, gain_col + g * PACK + t : gain_col + g * PACK + t + 1],
                    bias=affine[:, shift_col + g * PACK + t : shift_col + g * PACK + t + 1],
                )
        keep_busy_mx(4)

        out_banks = [
            acc.tile([P, WO_GROUP, P], F32, name="out_bank%d" % n, tag="acc") for n in range(n_wo_groups)
        ]
        h2_codes = mx.tile([P, PASSES * P], U32, name="h2_codes", align_bytes=64)
        h2_scales = mx.tile([P, PASSES * P], U8, name="h2_scales", align_bytes=64)
        h2_grouped = [
            work.tile([P, P, PACK], BF16, name="h2_grouped%d" % g, align_bytes=64) for g in range(PASSES)
        ]
        for g in range(PASSES):
            nc.vector.tensor_copy(
                out=h2_grouped[g][:].rearrange("p (c i) t -> p c t i", i=RUN),
                in_=h2_flipped[g][:].rearrange("p t (c i) -> p c t i", i=RUN),
            )
        for g in range(PASSES):
            nc.vector.quantize_mx(
                out=h2_codes[:, g * P : (g + 1) * P].bitcast(FP8X4),
                scales=h2_scales[:, g * P : (g + 1) * P],
                in_=h2_grouped[g][:].rearrange("p r t -> p (r t)"),
            )
        for n in range(n_wo_groups):
            for g in range(PASSES):
                multiply(out_banks[n][:], (h2_codes, h2_scales), wo_mx[n], g, WO_GROUP * P)

        out_sb = work.tile([P, OUT], F32, name="out_sb")
        for n in range(n_wo_groups):
            cols = slice(n * WO_GROUP * P, (n + 1) * WO_GROUP * P)
            nc.vector.tensor_tensor(
                out=out_sb[:, cols],
                in0=out_banks[n][:].rearrange("p b q -> p (b q)"),
                in1=bo_all[:, cols],
                op=ALU.add,
            )
            nc.sync.dma_start(out=out[:, cols], in_=out_sb[:, cols])
